import numpy as np
import ml_dtypes


def mxq(x, axis, fmt="e4m3"):
    dtype, down = {"e4m3": (ml_dtypes.float8_e4m3fn, 7), "e5m2": (ml_dtypes.float8_e5m2, 14)}[fmt]
    v = np.moveaxis(np.asarray(x, np.float32).astype(ml_dtypes.bfloat16).astype(np.float64), axis, -1)
    blocks = v.reshape(v.shape[:-1] + (-1, 32))
    amax = np.abs(blocks).max(-1, keepdims=True)
    byte = np.maximum(np.where(amax > 0, np.frexp(amax)[1] - 1 + 127, 0) - down, 1)
    scale = np.exp2(byte - 127.0)
    codes = (blocks / scale).astype(np.float32).astype(dtype).astype(np.float64)
    return np.moveaxis((codes * scale).reshape(v.shape), -1, axis)


WIDE = False


def mx_kscale(k):
    if not WIDE:
        return np.ones(k)
    levels = np.array([10, -10, 5, -5, 0])
    a = np.random.permutation(np.resize(levels, k // 512 * 4)).reshape(k // 512, 4)
    idx = np.arange(k)
    return np.exp2(a[idx // 512, idx % 128 // 32])


BF16 = ml_dtypes.bfloat16


def bf(x):
    return np.asarray(x, np.float32).astype(BF16)


def f64(x):
    return np.asarray(x).astype(np.float64)


E2M1 = np.array([0.0, 0.5, 1.0, 1.5, 2.0, 3.0, 4.0, 6.0, -0.0, -0.5, -1.0, -1.5, -2.0, -3.0, -4.0, -6.0])


def pack_weight(w, fmt):
    k, n = w.shape
    w = f64(bf(w)).reshape(k // 32, 32, n)
    amax = np.abs(w).max(1)
    if fmt == "e4m3":
        byte = np.frexp(amax)[1] - 1 + 127 - 7
    else:
        mant, ex = np.frexp(amax / 6.0)
        byte = np.where(mant > 0.5, ex, ex - 1) + 127
    byte = np.clip(np.where(amax > 0, byte, 1), 1, 254)
    scaled = (w * np.exp2(127.0 - byte)[:, None, :]).reshape(k, n).astype(np.float32)
    by_word = np.ascontiguousarray(scaled.reshape(k // 512, 128, 4, n).transpose(0, 1, 3, 2))
    if fmt == "e4m3":
        words = by_word.astype(ml_dtypes.float8_e4m3fn).view(np.uint8)
    else:
        c = by_word.astype(ml_dtypes.float4_e2m1fn).view(np.uint8) & 0xF
        words = c[..., 0::2] | (c[..., 1::2] << 4)
    return np.ascontiguousarray(words), np.ascontiguousarray(byte.astype(np.uint8).reshape(k // 512, 16, n))


def unpack_weight(words, scales, fmt):
    g, p, n, _ = words.shape
    if fmt == "e4m3":
        vals = np.ascontiguousarray(words).view(ml_dtypes.float8_e4m3fn).astype(np.float64)
    else:
        nib = np.empty((g, p, n, 4), np.uint8)
        nib[..., 0::2] = words & 0xF
        nib[..., 1::2] = words >> 4
        vals = E2M1[nib]
    vals = vals * np.repeat(np.exp2(scales.astype(np.float64) - 127.0), 8, axis=1)[..., None]
    return vals.transpose(0, 1, 3, 2).reshape(g * 512, n)


B, C, T, P, N, D = 8, 16, 2048, 128, 8, 512
L = T // P
G = L // N
FMT = 'e4m3'


def gelu_tanh(v):
    return 0.5 * v * (1.0 + np.tanh(np.sqrt(2.0 / np.pi) * (v + 0.044715 * v**3)))


def setup_inputs():
    s = mx_kscale(D)
    x = bf(np.random.standard_normal((B, C, T)))
    emb_W = bf(np.random.standard_normal((P, D)) / np.sqrt(P) * s)
    emb_b = bf(np.random.standard_normal(D) * 0.2 * s)
    w1 = np.random.standard_normal((N, D, D)) / np.sqrt(D) / s[None, :, None]
    enc_b1 = bf(np.random.standard_normal((N, D)) * 0.2)
    w2 = np.random.standard_normal((N, D, D)) / np.sqrt(D)
    enc_b2 = bf(np.random.standard_normal((N, D)) * 0.2)
    w1_words, w1_scales = pack_weight(w1.reshape(-1, D), FMT)
    w2_words, w2_scales = pack_weight(w2.reshape(-1, D), FMT)
    return {'x': x,
            'emb_W': emb_W,
            'emb_b': emb_b,
            'enc_W1_words': w1_words,
            'enc_W1_scales': w1_scales,
            'enc_b1': enc_b1,
            'enc_W2_words': w2_words,
            'enc_W2_scales': w2_scales,
            'enc_b2': enc_b2}


def reference(x, emb_W, emb_b, enc_W1_words, enc_W1_scales, enc_b1, enc_W2_words, enc_W2_scales, enc_b2):
    e = f64(x).reshape(B * C * L, P) @ f64(emb_W) + f64(emb_b)
    e = np.moveaxis(e.reshape(B, C, G, N, D), 3, 0).reshape(N, B * C * G, D)
    a = (mxq(e, 2, 'e4m3') @ unpack_weight(enc_W1_words, enc_W1_scales, FMT).reshape(N, D, D)) + f64(enc_b1)[:, None, :]
    g = gelu_tanh(a)
    o = (mxq(g, 2, 'e4m3') @ unpack_weight(enc_W2_words, enc_W2_scales, FMT).reshape(N, D, D)) + f64(enc_b2)[:, None, :]
    return o.reshape(N, B, C, G, D)

@@ -1,0 +1,266 @@
+from contextlib import ExitStack
+
+import concourse.mybir as mybir
+from concourse.masks import make_identity
+
+F32 = mybir.dt.float32
+BF16 = mybir.dt.bfloat16
+I32 = mybir.dt.int32
+U32 = mybir.dt.uint32
+U8 = mybir.dt.uint8
+FP8X4 = mybir.dt.float8_e4m3fn_x4
+ADD = mybir.AluOpType.add
+MULT = mybir.AluOpType.mult
+IDENTITY = mybir.ActivationFunctionType.Identity
+GELU = mybir.ActivationFunctionType.Gelu_apprx_tanh
+
+P = 128
+PACK = 4
+D = P * PACK
+MODELS = 8
+PATCHES = 2
+TOKENS = P * PATCHES
+PAIRS = MODELS // 2
+QUADRANTS = 4
+
+FLOPS = 2 * MODELS * TOKENS * (P * D + 2 * D * D)
+
+
+def tile_model_pa_e_kernel(
+    tc, x, emb_W, emb_b, enc_W1_words, enc_W1_scales, enc_b1, enc_W2_words, enc_W2_scales, enc_b2, out
+):
+    nc = tc.nc
+    with ExitStack() as ctx:
+        ctx.enter_context(tc.manual_schedule())
+        keep = ctx.enter_context(tc.tile_pool(name="keep", bufs=1))
+        stage = ctx.enter_context(tc.tile_pool(name="stage", bufs=2))
+        sums = ctx.enter_context(tc.tile_pool(name="sums", bufs=4))
+        psum_v = ctx.enter_context(tc.psum_pool(name="psum_v", bufs=4))
+        psum_s = ctx.enter_context(tc.psum_pool(name="psum_s", bufs=4))
+
+        warm = keep.tile([P, 1], F32)
+        nc.vector.memset(warm[:], 0.0)
+        w_scales = keep.tile([P, 2, MODELS, D], U8, align_bytes=64)
+        nc.vector.memset(w_scales[:].rearrange("p w g c -> p (w g c)").bitcast(I32), 0)
+        w_words = keep.tile([P, 2, MODELS, D], U32, align_bytes=64)
+        biases = keep.tile([P, 2, MODELS, D], BF16)
+
+        def load_scales(layer, scales):
+            for quadrant in range(QUADRANTS):
+                nc.sync.dma_start(
+                    out=w_scales[32 * quadrant : 32 * quadrant + 4, layer].bitcast(I32),
+                    in_=scales.bitcast(I32)[:, 4 * quadrant : 4 * quadrant + 4, :].rearrange("g r c -> r g c"),
+                )
+
+        def load_words(layer, words, n):
+            nc.sync.dma_start(
+                out=w_words[:, layer, n, :].bitcast(I32),
+                in_=words[n].rearrange("p c t -> p (c t)").bitcast(I32),
+            )
+
+        def load_biases(layer, bias, half):
+            models = slice(4 * half, 4 * (half + 1))
+            nc.sync.dma_start(
+                out=biases[:, layer, models, :].rearrange("p n d -> p (n d)"),
+                in_=bias[models, :].rearrange("n d -> (n d)").partition_broadcast(P),
+            )
+
+        x_sb = keep.tile([P, MODELS * TOKENS], BF16)
+        nc.sync.dma_start(out=x_sb[:], in_=x.rearrange("b c t -> (b c) t"))
+        emb_w_sb = keep.tile([P, D], BF16)
+        nc.sync.dma_start(out=emb_w_sb[:], in_=emb_W)
+        emb_b_bf = keep.tile([P, PACK], BF16)
+        nc.sync.dma_start(out=emb_b_bf[:], in_=emb_b.rearrange("(p t) -> p t", t=PACK))
+        load_biases(0, enc_b1, 0)
+        load_scales(0, enc_W1_scales)
+        load_words(0, enc_W1_words, 0)
+        load_biases(1, enc_b2, 0)
+        load_scales(1, enc_W2_scales)
+        load_words(1, enc_W2_words, 0)
+        for n in range(1, MODELS):
+            if n == MODELS // 2:
+                load_biases(0, enc_b1, 1)
+                load_biases(1, enc_b2, 1)
+            load_words(0, enc_W1_words, n)
+            load_words(1, enc_W2_words, n)
+
+        nc.scalar.activation(out=warm[:], in_=warm[:], func=GELU)
+        ident_bf = keep.tile([P, P], BF16)
+        make_identity(nc, ident_bf[:])
+        ident_f32 = keep.tile([P, P], F32)
+        make_identity(nc, ident_f32[:])
+        emb_b_col = keep.tile([P, PACK], F32)
+        nc.vector.tensor_copy(out=emb_b_col[:], in_=emb_b_bf[:])
+        emb_w_sorted = keep.tile([P, PACK, P], BF16)
+        nc.vector.tensor_copy(out=emb_w_sorted[:], in_=emb_w_sb[:].rearrange("s (p t) -> s t p", t=PACK))
+
+        x_t = keep.tile([P, MODELS * TOKENS], BF16)
+        e_codes = keep.tile([P, MODELS * TOKENS], U32, align_bytes=64)
+        e_scales = keep.tile([P, MODELS * TOKENS], U8, align_bytes=64)
+
+        def transpose_x(pair):
+            x_t_ps = psum_s.tile([P, 2 * PATCHES, P], BF16, tag="s")
+            for m in range(2):
+                for l in range(PATCHES):
+                    patch = MODELS * l + 2 * pair + m
+                    nc.tensor.transpose(
+                        out=x_t_ps[:, PATCHES * m + l, :],
+                        in_=x_sb[:, P * patch : P * (patch + 1)],
+                        identity=ident_bf[:],
+                    )
+            nc.scalar.copy(
+                out=x_t[:, 2 * TOKENS * pair : 2 * TOKENS * (pair + 1)], in_=x_t_ps[:].rearrange("s a b -> s (a b)")
+            )
+
+        def embed_by_token(n):
+            banks = []
+            for l in range(PATCHES):
+                e_ps = psum_v.tile([P, PACK, P], F32, tag="v")
+                first = TOKENS * n + P * l
+                for t in range(PACK):
+                    nc.tensor.matmul(
+                        out=e_ps[:, t, :],
+                        lhsT=emb_w_sorted[:, t, :],
+                        rhs=x_t[:, first : first + P],
+                        start=True,
+                        stop=True,
+                    )
+                banks.append(e_ps)
+            return banks
+
+        def quantise_by_token(n, banks):
+            e_words = stage.tile([P, PATCHES, P, PACK], BF16, align_bytes=64)
+            for l in range(PATCHES):
+                nc.vector.tensor_tensor(
+                    out=e_words[:, l],
+                    in0=banks[l][:].rearrange("p t w -> p w t"),
+                    in1=emb_b_col[:].unsqueeze(1).to_broadcast([P, P, PACK]),
+                    op=ADD,
+                )
+            nc.vector.quantize_mx(
+                out=e_codes[:, TOKENS * n : TOKENS * (n + 1)].bitcast(FP8X4),
+                scales=e_scales[:, TOKENS * n : TOKENS * (n + 1)],
+                in_=e_words[:].rearrange("p l w t -> p (l w t)"),
+            )
+
+        def embed_planes(pair, e_planes, first_t):
+            for t in (first_t, first_t + 1):
+                e_ps = psum_s.tile([P, 2 * TOKENS], F32, tag="s")
+                nc.tensor.matmul(
+                    out=e_ps[:],
+                    lhsT=emb_w_sorted[:, t, :],
+                    rhs=x_t[:, 2 * TOKENS * pair : 2 * TOKENS * (pair + 1)],
+                    start=True,
+                    stop=True,
+                )
+                nc.scalar.activation(
+                    out=e_planes[:, t, :], in_=e_ps[:], func=IDENTITY, bias=emb_b_col[:, t : t + 1], scale=1.0
+                )
+
+        def regroup(e_planes):
+            e_grouped = stage.tile([P, 2 * TOKENS, PACK], BF16, align_bytes=64)
+            nc.gpsimd.tensor_scalar(
+                out=e_grouped[:],
+                in0=e_planes[:].rearrange("p t w -> p w t"),
+                scalar1=1.0,
+                scalar2=0.0,
+                op0=MULT,
+                op1=ADD,
+            )
+            return e_grouped
+
+        def quantise_pair(pair, e_grouped):
+            nc.vector.quantize_mx(
+                out=e_codes[:, 2 * TOKENS * pair : 2 * TOKENS * (pair + 1)].bitcast(FP8X4),
+                scales=e_scales[:, 2 * TOKENS * pair : 2 * TOKENS * (pair + 1)],
+                in_=e_grouped[:].rearrange("p w t -> p (w t)"),
+            )
+
+        def first_product(n):
+            sorted_sums = []
+            for l in range(PATCHES):
+                tokens = slice(TOKENS * n + P * l, TOKENS * n + P * (l + 1))
+                a_ps = psum_v.tile([P, D], F32, tag="v")
+                nc.tensor.matmul_mx(
+                    out=a_ps[:],
+                    lhsT=e_codes[:, tokens].bitcast(FP8X4),
+                    lhsT_scale=e_scales[:, tokens],
+                    rhs=w_words[:, 0, n, :].bitcast(FP8X4),
+                    rhs_scale=w_scales[:, 0, n, :],
+                    start=True,
+                    stop=True,
+                )
+                a_sorted = sums.tile([P, PACK, P], F32)
+                nc.vector.tensor_tensor(
+                    out=a_sorted[:],
+                    in0=a_ps[:].rearrange("w (p t) -> w t p", t=PACK),
+                    in1=biases[:, 0, n, :].rearrange("w (p t) -> w t p", t=PACK),
+                    op=ADD,
+                )
+                sorted_sums.append(a_sorted)
+            return sorted_sums
+
+        def hidden(sorted_sums):
+            g_grouped = stage.tile([P, PATCHES, P, PACK], BF16, align_bytes=64)
+            for l in range(PATCHES):
+                a_t_ps = psum_s.tile([P, PACK, P], F32, tag="s")
+                for t in range(PACK):
+                    nc.tensor.transpose(out=a_t_ps[:, t, :], in_=sorted_sums[l][:, t, :], identity=ident_f32[:])
+                nc.scalar.activation(out=g_grouped[:, l], in_=a_t_ps[:].rearrange("p t w -> p w t"), func=GELU)
+            g_codes = stage.tile([P, TOKENS], U32, align_bytes=64)
+            g_scales = stage.tile([P, TOKENS], U8, align_bytes=64)
+            nc.vector.quantize_mx(
+                out=g_codes[:].bitcast(FP8X4),
+                scales=g_scales[:],
+                in_=g_grouped[:].rearrange("p l w t -> p (l w t)"),
+            )
+            return g_codes, g_scales
+
+        def second_product(n, g_codes, g_scales):
+            for l in range(PATCHES):
+                o_ps = psum_v.tile([P, D], F32, tag="v")
+                nc.tensor.matmul_mx(
+                    out=o_ps[:],
+                    lhsT=g_codes[:, P * l : P * (l + 1)].bitcast(FP8X4),
+                    lhsT_scale=g_scales[:, P * l : P * (l + 1)],
+                    rhs=w_words[:, 1, n, :].bitcast(FP8X4),
+                    rhs_scale=w_scales[:, 1, n, :],
+                    start=True,
+                    stop=True,
+                )
+                o_sb = sums.tile([P, D], F32)
+                nc.vector.tensor_tensor(out=o_sb[:], in0=o_ps[:], in1=biases[:, 1, n, :], op=ADD)
+                nc.sync.dma_start(out=out[n, :, :, l, :].rearrange("b c d -> (b c) d"), in_=o_sb[:])
+
+        transpose_x(0)
+        transpose_x(1)
+        quantise_by_token(0, embed_by_token(0))
+        planes = {}
+        grouped = {}
+        planes[1] = stage.tile([P, PACK, 2 * TOKENS], BF16, name="e_planes", tag="e_planes")
+        embed_planes(1, planes[1], 0)
+        embed_planes(1, planes[1], 2)
+        grouped[1] = regroup(planes[1])
+
+        g_codes, g_scales = None, None
+        for s in range(MODELS + 1):
+            if s < MODELS:
+                sorted_sums = first_product(s)
+            if s == 0:
+                banks = embed_by_token(1)
+                transpose_x(2)
+                transpose_x(3)
+                quantise_by_token(1, banks)
+            else:
+                second_product(s - 1, g_codes, g_scales)
+            if s % 2 == 1 and (s + 1) // 2 < PAIRS:
+                quantise_pair((s + 1) // 2, grouped[(s + 1) // 2])
+            if s < MODELS:
+                g_codes, g_scales = hidden(sorted_sums)
+            pair = s // 2 + 2
+            if pair < PAIRS:
+                if s % 2 == 0:
+                    planes[pair] = stage.tile([P, PACK, 2 * TOKENS], BF16, name="e_planes", tag="e_planes")
+                embed_planes(pair, planes[pair], 2 * (s % 2))
+                if s % 2 == 1:
+                    grouped[pair] = regroup(planes[pair])

@@ -40,10 +40,11 @@ def tile_model_pa_e_kernel(
 
         warm = keep.tile([P, 1], F32)
         nc.vector.memset(warm[:], 0.0)
+        bias_rows = keep.tile([P, P], BF16)
+        nc.vector.memset(bias_rows[:], 0.0)
         w_scales = keep.tile([P, 2, MODELS, D], U8, align_bytes=64)
         nc.vector.memset(w_scales[:].rearrange("p w g c -> p (w g c)").bitcast(I32), 0)
         w_words = keep.tile([P, 2, MODELS, D], U32, align_bytes=64)
-        biases = keep.tile([P, 2, MODELS, D], BF16)
 
         def load_scales(layer, scales):
             for quadrant in range(QUADRANTS):
@@ -58,29 +59,19 @@ def tile_model_pa_e_kernel(
                 in_=words[n].rearrange("p c t -> p (c t)").bitcast(I32),
             )
 
-        def load_biases(layer, bias, half):
-            models = slice(4 * half, 4 * (half + 1))
-            nc.sync.dma_start(
-                out=biases[:, layer, models, :].rearrange("p n d -> p (n d)"),
-                in_=bias[models, :].rearrange("n d -> (n d)").partition_broadcast(P),
-            )
-
         x_sb = keep.tile([P, MODELS * TOKENS], BF16)
         nc.sync.dma_start(out=x_sb[:], in_=x.rearrange("b c t -> (b c) t"))
+        nc.sync.dma_start(out=bias_rows[0:32, :], in_=enc_b1.rearrange("n (c p) -> (n c) p", p=P))
+        nc.sync.dma_start(out=bias_rows[32:64, :], in_=enc_b2.rearrange("n (c p) -> (n c) p", p=P))
         emb_w_sb = keep.tile([P, D], BF16)
         nc.sync.dma_start(out=emb_w_sb[:], in_=emb_W)
         emb_b_bf = keep.tile([P, PACK], BF16)
         nc.sync.dma_start(out=emb_b_bf[:], in_=emb_b.rearrange("(p t) -> p t", t=PACK))
-        load_biases(0, enc_b1, 0)
         load_scales(0, enc_W1_scales)
         load_words(0, enc_W1_words, 0)
-        load_biases(1, enc_b2, 0)
         load_scales(1, enc_W2_scales)
         load_words(1, enc_W2_words, 0)
         for n in range(1, MODELS):
-            if n == MODELS // 2:
-                load_biases(0, enc_b1, 1)
-                load_biases(1, enc_b2, 1)
             load_words(0, enc_W1_words, n)
             load_words(1, enc_W2_words, n)
 
@@ -97,6 +88,29 @@ def tile_model_pa_e_kernel(
         x_t = keep.tile([P, MODELS * TOKENS], BF16)
         e_codes = keep.tile([P, MODELS * TOKENS], U32, align_bytes=64)
         e_scales = keep.tile([P, MODELS * TOKENS], U8, align_bytes=64)
+
+        bias_col = keep.tile([P, 64], BF16)
+
+        def transpose_bias_rows():
+            bias_col_ps = psum_s.tile([P, P], BF16, tag="s")
+            nc.tensor.transpose(out=bias_col_ps[:], in_=bias_rows[:], identity=ident_bf[:])
+            nc.scalar.copy(out=bias_col[:], in_=bias_col_ps[:, 0:64])
+
+        def broadcast_biases(s):
+            bias_ps = psum_s.tile([P, 2, D], BF16, tag="s")
+            step_biases = sums.tile([P, 2, D], BF16)
+            for layer in range(2):
+                n = s - layer
+                if 0 <= n < MODELS:
+                    for c in range(D // P):
+                        r = 32 * layer + 4 * n + c
+                        nc.tensor.transpose(
+                            out=bias_ps[:, layer, P * c : P * (c + 1)],
+                            in_=bias_col[:, r : r + 1].to_broadcast([P, P]),
+                            identity=ident_bf[:],
+                        )
+                    nc.scalar.copy(out=step_biases[:, layer, :], in_=bias_ps[:, layer, :])
+            return step_biases
 
         def transpose_x(pair):
             x_t_ps = psum_s.tile([P, 2 * PATCHES, P], BF16, tag="s")
@@ -176,7 +190,7 @@ def tile_model_pa_e_kernel(
                 in_=e_grouped[:].rearrange("p w t -> p (w t)"),
             )
 
-        def first_product(n):
+        def first_product(n, step_biases):
             sorted_sums = []
             for l in range(PATCHES):
                 tokens = slice(TOKENS * n + P * l, TOKENS * n + P * (l + 1))
@@ -194,7 +208,7 @@ def tile_model_pa_e_kernel(
                 nc.vector.tensor_tensor(
                     out=a_sorted[:],
                     in0=a_ps[:].rearrange("w (p t) -> w t p", t=PACK),
-                    in1=biases[:, 0, n, :].rearrange("w (p t) -> w t p", t=PACK),
+                    in1=step_biases[:, 0, :].rearrange("w (p t) -> w t p", t=PACK),
                     op=ADD,
                 )
                 sorted_sums.append(a_sorted)
@@ -216,7 +230,7 @@ def tile_model_pa_e_kernel(
             )
             return g_codes, g_scales
 
-        def second_product(n, g_codes, g_scales):
+        def second_product(n, step_biases, g_codes, g_scales):
             for l in range(PATCHES):
                 o_ps = psum_v.tile([P, D], F32, tag="v")
                 nc.tensor.matmul_mx(
@@ -229,9 +243,11 @@ def tile_model_pa_e_kernel(
                     stop=True,
                 )
                 o_sb = sums.tile([P, D], F32)
-                nc.vector.tensor_tensor(out=o_sb[:], in0=o_ps[:], in1=biases[:, 1, n, :], op=ADD)
+                nc.vector.tensor_tensor(out=o_sb[:], in0=o_ps[:], in1=step_biases[:, 1, :], op=ADD)
                 nc.sync.dma_start(out=out[n, :, :, l, :].rearrange("b c d -> (b c) d"), in_=o_sb[:])
 
+        transpose_bias_rows()
+        step_biases = broadcast_biases(0)
         transpose_x(0)
         transpose_x(1)
         quantise_by_token(0, embed_by_token(0))
@@ -245,18 +261,19 @@ def tile_model_pa_e_kernel(
         g_codes, g_scales = None, None
         for s in range(MODELS + 1):
             if s < MODELS:
-                sorted_sums = first_product(s)
+                sorted_sums = first_product(s, step_biases)
             if s == 0:
                 banks = embed_by_token(1)
                 transpose_x(2)
                 transpose_x(3)
                 quantise_by_token(1, banks)
             else:
-                second_product(s - 1, g_codes, g_scales)
+                second_product(s - 1, step_biases, g_codes, g_scales)
             if s % 2 == 1 and (s + 1) // 2 < PAIRS:
                 quantise_pair((s + 1) // 2, grouped[(s + 1) // 2])
             if s < MODELS:
                 g_codes, g_scales = hidden(sorted_sums)
+                step_biases = broadcast_biases(s + 1)
             pair = s // 2 + 2
             if pair < PAIRS:
                 if s % 2 == 0:

@@ -22,6 +22,7 @@ PATCHES = 2
 TOKENS = P * PATCHES
 PAIRS = MODELS // 2
 QUADRANTS = 4
+STEPS = MODELS + 2
 
 FLOPS = 2 * MODELS * TOKENS * (P * D + 2 * D * D)
 
@@ -59,21 +60,25 @@ def tile_model_pa_e_kernel(
                 in_=words[n].rearrange("p c t -> p (c t)").bitcast(I32),
             )
 
-        x_sb = keep.tile([P, MODELS * TOKENS], BF16)
-        nc.sync.dma_start(out=x_sb[:], in_=x.rearrange("b c t -> (b c) t"))
-        nc.sync.dma_start(out=bias_rows[0:32, :], in_=enc_b1.rearrange("n (c p) -> (n c) p", p=P))
-        nc.sync.dma_start(out=bias_rows[32:64, :], in_=enc_b2.rearrange("n (c p) -> (n c) p", p=P))
+        x_sb = keep.tile([P, PATCHES, MODELS * P], BF16)
+        x_rows = x.rearrange("b c (l t) -> (b c) l t", l=PATCHES)
+        nc.sync.dma_start(out=x_sb[:, :, 0 : 2 * P], in_=x_rows[:, :, 0 : 2 * P])
         emb_w_sb = keep.tile([P, D], BF16)
         nc.sync.dma_start(out=emb_w_sb[:], in_=emb_W)
         emb_b_bf = keep.tile([P, PACK], BF16)
         nc.sync.dma_start(out=emb_b_bf[:], in_=emb_b.rearrange("(p t) -> p t", t=PACK))
+        nc.sync.dma_start(out=x_sb[:, :, 2 * P :], in_=x_rows[:, :, 2 * P :])
+        nc.sync.dma_start(out=bias_rows[0:32, :], in_=enc_b1.rearrange("n (c p) -> (n c) p", p=P))
+        nc.sync.dma_start(out=bias_rows[32:64, :], in_=enc_b2.rearrange("n (c p) -> (n c) p", p=P))
         load_scales(0, enc_W1_scales)
         load_words(0, enc_W1_words, 0)
+        load_words(0, enc_W1_words, 1)
         load_scales(1, enc_W2_scales)
         load_words(1, enc_W2_words, 0)
-        for n in range(1, MODELS):
+        for n in range(2, MODELS):
             load_words(0, enc_W1_words, n)
-            load_words(1, enc_W2_words, n)
+            load_words(1, enc_W2_words, n - 1)
+        load_words(1, enc_W2_words, MODELS - 1)
 
         nc.scalar.activation(out=warm[:], in_=warm[:], func=GELU)
         ident_bf = keep.tile([P, P], BF16)
@@ -97,30 +102,28 @@ def tile_model_pa_e_kernel(
             nc.scalar.copy(out=bias_col[:], in_=bias_col_ps[:, 0:64])
 
         def broadcast_biases(s):
+            layers = [layer for layer in range(2) if 0 <= s - 2 * layer < MODELS]
             bias_ps = psum_s.tile([P, 2, D], BF16, tag="s")
+            for layer in layers:
+                for c in range(D // P):
+                    r = 32 * layer + 4 * (s - 2 * layer) + c
+                    nc.tensor.transpose(
+                        out=bias_ps[:, layer, P * c : P * (c + 1)],
+                        in_=bias_col[:, r : r + 1].to_broadcast([P, P]),
+                        identity=ident_bf[:],
+                    )
             step_biases = sums.tile([P, 2, D], BF16)
-            for layer in range(2):
-                n = s - layer
-                if 0 <= n < MODELS:
-                    for c in range(D // P):
-                        r = 32 * layer + 4 * n + c
-                        nc.tensor.transpose(
-                            out=bias_ps[:, layer, P * c : P * (c + 1)],
-                            in_=bias_col[:, r : r + 1].to_broadcast([P, P]),
-                            identity=ident_bf[:],
-                        )
-                    nc.scalar.copy(out=step_biases[:, layer, :], in_=bias_ps[:, layer, :])
+            written = slice(layers[0], layers[-1] + 1)
+            nc.scalar.copy(out=step_biases[:, written, :], in_=bias_ps[:, written, :])
             return step_biases
 
         def transpose_x(pair):
             x_t_ps = psum_s.tile([P, 2 * PATCHES, P], BF16, tag="s")
             for m in range(2):
                 for l in range(PATCHES):
-                    patch = MODELS * l + 2 * pair + m
+                    n = 2 * pair + m
                     nc.tensor.transpose(
-                        out=x_t_ps[:, PATCHES * m + l, :],
-                        in_=x_sb[:, P * patch : P * (patch + 1)],
-                        identity=ident_bf[:],
+                        out=x_t_ps[:, PATCHES * m + l, :], in_=x_sb[:, l, P * n : P * (n + 1)], identity=ident_bf[:]
                     )
             nc.scalar.copy(
                 out=x_t[:, 2 * TOKENS * pair : 2 * TOKENS * (pair + 1)], in_=x_t_ps[:].rearrange("s a b -> s (a b)")
@@ -142,22 +145,19 @@ def tile_model_pa_e_kernel(
                 banks.append(e_ps)
             return banks
 
-        def quantise_by_token(n, banks):
-            e_words = stage.tile([P, PATCHES, P, PACK], BF16, align_bytes=64)
+        def words_from_psum(banks):
+            e_words = sums.tile([P, TOKENS, PACK], BF16, align_bytes=64)
             for l in range(PATCHES):
                 nc.vector.tensor_tensor(
-                    out=e_words[:, l],
+                    out=e_words[:, P * l : P * (l + 1), :],
                     in0=banks[l][:].rearrange("p t w -> p w t"),
                     in1=emb_b_col[:].unsqueeze(1).to_broadcast([P, P, PACK]),
                     op=ADD,
                 )
-            nc.vector.quantize_mx(
-                out=e_codes[:, TOKENS * n : TOKENS * (n + 1)].bitcast(FP8X4),
-                scales=e_scales[:, TOKENS * n : TOKENS * (n + 1)],
-                in_=e_words[:].rearrange("p l w t -> p (l w t)"),
-            )
+            return e_words
 
-        def embed_planes(pair, e_planes, first_t):
+        def embed_planes(pair, first_t):
+            banks = []
             for t in (first_t, first_t + 1):
                 e_ps = psum_s.tile([P, 2 * TOKENS], F32, tag="s")
                 nc.tensor.matmul(
@@ -167,60 +167,68 @@ def tile_model_pa_e_kernel(
                     start=True,
                     stop=True,
                 )
+                banks.append(e_ps)
+            return banks
+
+        def round_planes(e_planes, first_t, banks):
+            for i in range(2):
+                t = first_t + i
                 nc.scalar.activation(
-                    out=e_planes[:, t, :], in_=e_ps[:], func=IDENTITY, bias=emb_b_col[:, t : t + 1], scale=1.0
+                    out=e_planes[:, t, :], in_=banks[i][:], func=IDENTITY, bias=emb_b_col[:, t : t + 1], scale=1.0
                 )
 
-        def regroup(e_planes):
-            e_grouped = stage.tile([P, 2 * TOKENS, PACK], BF16, align_bytes=64)
+        def words_from_planes(e_planes, m):
+            e_words = sums.tile([P, TOKENS, PACK], BF16, align_bytes=64)
             nc.gpsimd.tensor_scalar(
-                out=e_grouped[:],
-                in0=e_planes[:].rearrange("p t w -> p w t"),
+                out=e_words[:],
+                in0=e_planes[:, :, TOKENS * m : TOKENS * (m + 1)].rearrange("p t w -> p w t"),
                 scalar1=1.0,
                 scalar2=0.0,
                 op0=MULT,
                 op1=ADD,
             )
-            return e_grouped
+            return e_words
 
-        def quantise_pair(pair, e_grouped):
+        def quantise_embedding(n, e_words):
             nc.vector.quantize_mx(
-                out=e_codes[:, 2 * TOKENS * pair : 2 * TOKENS * (pair + 1)].bitcast(FP8X4),
-                scales=e_scales[:, 2 * TOKENS * pair : 2 * TOKENS * (pair + 1)],
-                in_=e_grouped[:].rearrange("p w t -> p (w t)"),
+                out=e_codes[:, TOKENS * n : TOKENS * (n + 1)].bitcast(FP8X4),
+                scales=e_scales[:, TOKENS * n : TOKENS * (n + 1)],
+                in_=e_words[:].rearrange("p w t -> p (w t)"),
             )
 
-        def first_product(n, step_biases):
-            sorted_sums = []
+        def multiply(codes, scales, layer, n):
+            banks = []
             for l in range(PATCHES):
-                tokens = slice(TOKENS * n + P * l, TOKENS * n + P * (l + 1))
-                a_ps = psum_v.tile([P, D], F32, tag="v")
+                product = psum_v.tile([P, D], F32, tag="v")
                 nc.tensor.matmul_mx(
-                    out=a_ps[:],
-                    lhsT=e_codes[:, tokens].bitcast(FP8X4),
-                    lhsT_scale=e_scales[:, tokens],
-                    rhs=w_words[:, 0, n, :].bitcast(FP8X4),
-                    rhs_scale=w_scales[:, 0, n, :],
+                    out=product[:],
+                    lhsT=codes[:, P * l : P * (l + 1)].bitcast(FP8X4),
+                    lhsT_scale=scales[:, P * l : P * (l + 1)],
+                    rhs=w_words[:, layer, n, :].bitcast(FP8X4),
+                    rhs_scale=w_scales[:, layer, n, :],
                     start=True,
                     stop=True,
                 )
-                a_sorted = sums.tile([P, PACK, P], F32)
-                nc.vector.tensor_tensor(
-                    out=a_sorted[:],
-                    in0=a_ps[:].rearrange("w (p t) -> w t p", t=PACK),
-                    in1=step_biases[:, 0, :].rearrange("w (p t) -> w t p", t=PACK),
-                    op=ADD,
-                )
-                sorted_sums.append(a_sorted)
-            return sorted_sums
+                banks.append(product)
+            return banks
 
-        def hidden(sorted_sums):
-            g_grouped = stage.tile([P, PATCHES, P, PACK], BF16, align_bytes=64)
-            for l in range(PATCHES):
-                a_t_ps = psum_s.tile([P, PACK, P], F32, tag="s")
-                for t in range(PACK):
-                    nc.tensor.transpose(out=a_t_ps[:, t, :], in_=sorted_sums[l][:, t, :], identity=ident_f32[:])
-                nc.scalar.activation(out=g_grouped[:, l], in_=a_t_ps[:].rearrange("p t w -> p w t"), func=GELU)
+        def add_b1(a_ps, step_biases):
+            a_sorted = sums.tile([P, PACK, P], F32)
+            nc.vector.tensor_tensor(
+                out=a_sorted[:],
+                in0=a_ps[:].rearrange("w (p t) -> w t p", t=PACK),
+                in1=step_biases[:, 0, :].rearrange("w (p t) -> w t p", t=PACK),
+                op=ADD,
+            )
+            return a_sorted
+
+        def gelu_transposed(a_sorted, g_words):
+            a_t_ps = psum_s.tile([P, PACK, P], F32, tag="s")
+            for t in range(PACK):
+                nc.tensor.transpose(out=a_t_ps[:, t, :], in_=a_sorted[:, t, :], identity=ident_f32[:])
+            nc.scalar.activation(out=g_words, in_=a_t_ps[:].rearrange("p t w -> p w t"), func=GELU)
+
+        def quantise_hidden(g_grouped):
             g_codes = stage.tile([P, TOKENS], U32, align_bytes=64)
             g_scales = stage.tile([P, TOKENS], U8, align_bytes=64)
             nc.vector.quantize_mx(
@@ -230,54 +238,68 @@ def tile_model_pa_e_kernel(
             )
             return g_codes, g_scales
 
-        def second_product(n, step_biases, g_codes, g_scales):
-            for l in range(PATCHES):
-                o_ps = psum_v.tile([P, D], F32, tag="v")
-                nc.tensor.matmul_mx(
-                    out=o_ps[:],
-                    lhsT=g_codes[:, P * l : P * (l + 1)].bitcast(FP8X4),
-                    lhsT_scale=g_scales[:, P * l : P * (l + 1)],
-                    rhs=w_words[:, 1, n, :].bitcast(FP8X4),
-                    rhs_scale=w_scales[:, 1, n, :],
-                    start=True,
-                    stop=True,
-                )
-                o_sb = sums.tile([P, D], F32)
-                nc.vector.tensor_tensor(out=o_sb[:], in0=o_ps[:], in1=step_biases[:, 1, :], op=ADD)
-                nc.sync.dma_start(out=out[n, :, :, l, :].rearrange("b c d -> (b c) d"), in_=o_sb[:])
+        def add_b2_and_store(n, l, o_ps, step_biases):
+            o_sb = sums.tile([P, D], F32)
+            nc.vector.tensor_tensor(out=o_sb[:], in0=o_ps[:], in1=step_biases[:, 1, :], op=ADD)
+            nc.sync.dma_start(out=out[n, :, :, l, :].rearrange("b c d -> (b c) d"), in_=o_sb[:])
+
+        def first_product(n):
+            tokens = slice(TOKENS * n, TOKENS * (n + 1))
+            return multiply(e_codes[:, tokens], e_scales[:, tokens], 0, n)
+
+        biases = {}
+        planes = {}
+        plane_banks = {}
+        e_words = {}
+        a_banks = {}
+        g_grouped = {}
+        o_banks = {}
 
         transpose_bias_rows()
-        step_biases = broadcast_biases(0)
         transpose_x(0)
         transpose_x(1)
-        quantise_by_token(0, embed_by_token(0))
-        planes = {}
-        grouped = {}
+        e_words[0] = words_from_psum(embed_by_token(0))
+        quantise_embedding(0, e_words[0])
+        e_words[1] = words_from_psum(embed_by_token(1))
+        transpose_x(2)
+        transpose_x(3)
+        biases[0] = broadcast_biases(0)
         planes[1] = stage.tile([P, PACK, 2 * TOKENS], BF16, name="e_planes", tag="e_planes")
-        embed_planes(1, planes[1], 0)
-        embed_planes(1, planes[1], 2)
-        grouped[1] = regroup(planes[1])
+        round_planes(planes[1], 0, embed_planes(1, 0))
+        a_banks[0] = first_product(0)
+        round_planes(planes[1], 2, embed_planes(1, 2))
+        for m in range(2):
+            e_words[2 + m] = words_from_planes(planes[1], m)
+        biases[1] = broadcast_biases(1)
 
-        g_codes, g_scales = None, None
-        for s in range(MODELS + 1):
+        for s in range(STEPS):
+            pair = (s - 1) // 2 + 2
+            if s >= 1 and pair < PAIRS:
+                round_planes(planes[pair], 2 * ((s - 1) % 2), plane_banks[s - 1])
+                if (s - 1) % 2 == 1:
+                    for m in range(2):
+                        e_words[2 * pair + m] = words_from_planes(planes[pair], m)
             if s < MODELS:
-                sorted_sums = first_product(s, step_biases)
-            if s == 0:
-                banks = embed_by_token(1)
-                transpose_x(2)
-                transpose_x(3)
-                quantise_by_token(1, banks)
-            else:
-                second_product(s - 1, step_biases, g_codes, g_scales)
-            if s % 2 == 1 and (s + 1) // 2 < PAIRS:
-                quantise_pair((s + 1) // 2, grouped[(s + 1) // 2])
+                g_grouped[s] = stage.tile([P, PATCHES, P, PACK], BF16, name="g_grouped", tag="g_grouped", align_bytes=64)
+                gelu_transposed(add_b1(a_banks[s][0], biases[s]), g_grouped[s][:, 0])
+                a_sorted = add_b1(a_banks[s][1], biases[s])
+            if s + 1 < MODELS:
+                quantise_embedding(s + 1, e_words[s + 1])
+            if s + 2 < STEPS:
+                biases[s + 2] = broadcast_biases(s + 2)
             if s < MODELS:
-                g_codes, g_scales = hidden(sorted_sums)
-                step_biases = broadcast_biases(s + 1)
+                gelu_transposed(a_sorted, g_grouped[s][:, 1])
+            if 1 <= s <= MODELS:
+                g_codes, g_scales = quantise_hidden(g_grouped[s - 1])
+            if s + 1 < MODELS:
+                a_banks[s + 1] = first_product(s + 1)
+            if 1 <= s <= MODELS:
+                o_banks[s - 1] = multiply(g_codes, g_scales, 1, s - 1)
+            if s >= 2:
+                for l in range(PATCHES):
+                    add_b2_and_store(s - 2, l, o_banks[s - 2][l], biases[s])
             pair = s // 2 + 2
             if pair < PAIRS:
                 if s % 2 == 0:
                     planes[pair] = stage.tile([P, PACK, 2 * TOKENS], BF16, name="e_planes", tag="e_planes")
-                embed_planes(pair, planes[pair], 2 * (s % 2))
-                if s % 2 == 1:
-                    grouped[pair] = regroup(planes[pair])
+                plane_banks[s] = embed_planes(pair, 2 * (s % 2))

@@ -67,9 +67,9 @@ def tile_model_pa_e_kernel(
         nc.sync.dma_start(out=emb_w_sb[:], in_=emb_W)
         emb_b_bf = keep.tile([P, PACK], BF16)
         nc.sync.dma_start(out=emb_b_bf[:], in_=emb_b.rearrange("(p t) -> p t", t=PACK))
-        nc.sync.dma_start(out=x_sb[:, :, 2 * P :], in_=x_rows[:, :, 2 * P :])
         nc.sync.dma_start(out=bias_rows[0:32, :], in_=enc_b1.rearrange("n (c p) -> (n c) p", p=P))
         nc.sync.dma_start(out=bias_rows[32:64, :], in_=enc_b2.rearrange("n (c p) -> (n c) p", p=P))
+        nc.sync.dma_start(out=x_sb[:, :, 2 * P :], in_=x_rows[:, :, 2 * P :])
         load_scales(0, enc_W1_scales)
         load_words(0, enc_W1_words, 0)
         load_words(0, enc_W1_words, 1)
@@ -178,16 +178,16 @@ def tile_model_pa_e_kernel(
                 )
 
         def words_from_planes(e_planes, m):
-            e_words = sums.tile([P, TOKENS, PACK], BF16, align_bytes=64)
+            e_regrouped = stage.tile([P, TOKENS, PACK], BF16, align_bytes=64, bufs=1)
             nc.gpsimd.tensor_scalar(
-                out=e_words[:],
+                out=e_regrouped[:],
                 in0=e_planes[:, :, TOKENS * m : TOKENS * (m + 1)].rearrange("p t w -> p w t"),
                 scalar1=1.0,
                 scalar2=0.0,
                 op0=MULT,
                 op1=ADD,
             )
-            return e_words
+            return e_regrouped
 
         def quantise_embedding(n, e_words):
             nc.vector.quantize_mx(
@@ -255,9 +255,9 @@ def tile_model_pa_e_kernel(
         g_grouped = {}
         o_banks = {}
 
-        transpose_bias_rows()
         transpose_x(0)
         transpose_x(1)
+        transpose_bias_rows()
         e_words[0] = words_from_psum(embed_by_token(0))
         quantise_embedding(0, e_words[0])
         e_words[1] = words_from_psum(embed_by_token(1))
@@ -268,29 +268,27 @@ def tile_model_pa_e_kernel(
         round_planes(planes[1], 0, embed_planes(1, 0))
         a_banks[0] = first_product(0)
         round_planes(planes[1], 2, embed_planes(1, 2))
-        for m in range(2):
-            e_words[2 + m] = words_from_planes(planes[1], m)
+        e_words[2] = words_from_planes(planes[1], 0)
         biases[1] = broadcast_biases(1)
 
         for s in range(STEPS):
             pair = (s - 1) // 2 + 2
             if s >= 1 and pair < PAIRS:
                 round_planes(planes[pair], 2 * ((s - 1) % 2), plane_banks[s - 1])
-                if (s - 1) % 2 == 1:
-                    for m in range(2):
-                        e_words[2 * pair + m] = words_from_planes(planes[pair], m)
             if s < MODELS:
                 g_grouped[s] = stage.tile([P, PATCHES, P, PACK], BF16, name="g_grouped", tag="g_grouped", align_bytes=64)
                 gelu_transposed(add_b1(a_banks[s][0], biases[s]), g_grouped[s][:, 0])
                 a_sorted = add_b1(a_banks[s][1], biases[s])
+            if 1 <= s <= MODELS:
+                g_codes, g_scales = quantise_hidden(g_grouped[s - 1])
             if s + 1 < MODELS:
                 quantise_embedding(s + 1, e_words[s + 1])
+            if 3 <= s + 2 < MODELS:
+                e_words[s + 2] = words_from_planes(planes[(s + 2) // 2], (s + 2) % 2)
             if s + 2 < STEPS:
                 biases[s + 2] = broadcast_biases(s + 2)
             if s < MODELS:
                 gelu_transposed(a_sorted, g_grouped[s][:, 1])
-            if 1 <= s <= MODELS:
-                g_codes, g_scales = quantise_hidden(g_grouped[s - 1])
             if s + 1 < MODELS:
                 a_banks[s + 1] = first_product(s + 1)
             if 1 <= s <= MODELS:

@@ -10,8 +10,6 @@ U32 = mybir.dt.uint32
 U8 = mybir.dt.uint8
 FP8X4 = mybir.dt.float8_e4m3fn_x4
 ADD = mybir.AluOpType.add
-MULT = mybir.AluOpType.mult
-IDENTITY = mybir.ActivationFunctionType.Identity
 GELU = mybir.ActivationFunctionType.Gelu_apprx_tanh
 
 P = 128
@@ -20,9 +18,11 @@ D = P * PACK
 MODELS = 8
 PATCHES = 2
 TOKENS = P * PATCHES
-PAIRS = MODELS // 2
 QUADRANTS = 4
-STEPS = MODELS + 2
+PLANES = 4
+B1_ROW, EMB_B_ROW, B2_ROW = 0, 32, 64
+
+SCALAR_EMBEDS = (4, 5, 6, 7,)
 
 FLOPS = 2 * MODELS * TOKENS * (P * D + 2 * D * D)
 
@@ -34,30 +34,35 @@ def tile_model_pa_e_kernel(
     with ExitStack() as ctx:
         ctx.enter_context(tc.manual_schedule())
         keep = ctx.enter_context(tc.tile_pool(name="keep", bufs=1))
-        stage = ctx.enter_context(tc.tile_pool(name="stage", bufs=2))
-        sums = ctx.enter_context(tc.tile_pool(name="sums", bufs=4))
-        psum_v = ctx.enter_context(tc.psum_pool(name="psum_v", bufs=4))
-        psum_s = ctx.enter_context(tc.psum_pool(name="psum_s", bufs=4))
+        stage = ctx.enter_context(tc.tile_pool(name="stage", bufs=3))
+        psum_a = ctx.enter_context(tc.psum_pool(name="psum_a", bufs=3))
+        psum_o = ctx.enter_context(tc.psum_pool(name="psum_o", bufs=2))
+        psum_e = ctx.enter_context(tc.psum_pool(name="psum_e", bufs=2))
+        psum_b = ctx.enter_context(tc.psum_pool(name="psum_b", bufs=1))
 
         warm = keep.tile([P, 1], F32)
         nc.vector.memset(warm[:], 0.0)
-        bias_rows = keep.tile([P, P], BF16)
-        nc.vector.memset(bias_rows[:], 0.0)
-        w_scales = keep.tile([P, 2, MODELS, D], U8, align_bytes=64)
-        nc.vector.memset(w_scales[:].rearrange("p w g c -> p (w g c)").bitcast(I32), 0)
-        w_words = keep.tile([P, 2, MODELS, D], U32, align_bytes=64)
+        rows = keep.tile([P, D], BF16)
+        nc.vector.memset(rows[:], 0.0)
+        raw_scales = keep.tile([P, 2, 2, D], U8, align_bytes=64)
+        nc.vector.memset(raw_scales[:].rearrange("p w g c -> p (w g c)").bitcast(I32), 0)
+        pick = keep.tile([P, P], BF16)
+        nc.vector.memset(pick[:], 0.0)
+        nc.vector.memset(pick[EMB_B_ROW : EMB_B_ROW + 1, :], 1.0)
 
-        def load_scales(layer, scales):
-            for quadrant in range(QUADRANTS):
+        words = keep.tile([P, 2, MODELS, D], I32, align_bytes=64)
+
+        def load_scales(layer, scales, half):
+            first = PLANES * half
+            for q in range(QUADRANTS):
                 nc.sync.dma_start(
-                    out=w_scales[32 * quadrant : 32 * quadrant + 4, layer].bitcast(I32),
-                    in_=scales.bitcast(I32)[:, 4 * quadrant : 4 * quadrant + 4, :].rearrange("g r c -> r g c"),
+                    out=raw_scales[32 * q : 32 * q + 4 * PLANES, layer, half, :].bitcast(I32),
+                    in_=scales[first : first + PLANES, 4 * q : 4 * q + 4, :].bitcast(I32),
                 )
 
-        def load_words(layer, words, n):
+        def load_words(layer, given, n):
             nc.sync.dma_start(
-                out=w_words[:, layer, n, :].bitcast(I32),
-                in_=words[n].rearrange("p c t -> p (c t)").bitcast(I32),
+                out=words[:, layer, n, :], in_=given[n].rearrange("p c t -> p (c t)").bitcast(I32)
             )
 
         x_sb = keep.tile([P, PATCHES, MODELS * P], BF16)
@@ -65,239 +70,237 @@ def tile_model_pa_e_kernel(
         nc.sync.dma_start(out=x_sb[:, :, 0 : 2 * P], in_=x_rows[:, :, 0 : 2 * P])
         emb_w_sb = keep.tile([P, D], BF16)
         nc.sync.dma_start(out=emb_w_sb[:], in_=emb_W)
-        emb_b_bf = keep.tile([P, PACK], BF16)
-        nc.sync.dma_start(out=emb_b_bf[:], in_=emb_b.rearrange("(p t) -> p t", t=PACK))
-        nc.sync.dma_start(out=bias_rows[0:32, :], in_=enc_b1.rearrange("n (c p) -> (n c) p", p=P))
-        nc.sync.dma_start(out=bias_rows[32:64, :], in_=enc_b2.rearrange("n (c p) -> (n c) p", p=P))
-        nc.sync.dma_start(out=x_sb[:, :, 2 * P :], in_=x_rows[:, :, 2 * P :])
-        load_scales(0, enc_W1_scales)
+        nc.scalar.dma_start(out=rows[EMB_B_ROW : EMB_B_ROW + 1, :], in_=emb_b.rearrange("(o d) -> o d", o=1))
+        nc.scalar.dma_start(out=rows[B1_ROW : B1_ROW + MODELS, :], in_=enc_b1)
+        nc.scalar.dma_start(out=rows[B2_ROW : B2_ROW + MODELS, :], in_=enc_b2)
+        nc.sync.dma_start(out=x_sb[:, :, 2 * P : 4 * P], in_=x_rows[:, :, 2 * P : 4 * P])
+        load_scales(0, enc_W1_scales, 0)
         load_words(0, enc_W1_words, 0)
         load_words(0, enc_W1_words, 1)
-        load_scales(1, enc_W2_scales)
+        nc.sync.dma_start(out=x_sb[:, :, 4 * P :], in_=x_rows[:, :, 4 * P :])
+        load_scales(1, enc_W2_scales, 0)
         load_words(1, enc_W2_words, 0)
-        for n in range(2, MODELS):
+        load_words(0, enc_W1_words, 2)
+        load_words(1, enc_W2_words, 1)
+        load_words(0, enc_W1_words, 3)
+        load_scales(0, enc_W1_scales, 1)
+        load_scales(1, enc_W2_scales, 1)
+        load_words(1, enc_W2_words, 2)
+        for n in range(4, MODELS):
             load_words(0, enc_W1_words, n)
             load_words(1, enc_W2_words, n - 1)
         load_words(1, enc_W2_words, MODELS - 1)
 
         nc.scalar.activation(out=warm[:], in_=warm[:], func=GELU)
-        ident_bf = keep.tile([P, P], BF16)
-        make_identity(nc, ident_bf[:])
-        ident_f32 = keep.tile([P, P], F32)
-        make_identity(nc, ident_f32[:])
-        emb_b_col = keep.tile([P, PACK], F32)
-        nc.vector.tensor_copy(out=emb_b_col[:], in_=emb_b_bf[:])
-        emb_w_sorted = keep.tile([P, PACK, P], BF16)
-        nc.vector.tensor_copy(out=emb_w_sorted[:], in_=emb_w_sb[:].rearrange("s (p t) -> s t p", t=PACK))
+        ident = keep.tile([P, P], BF16)
+        make_identity(nc, ident[:])
 
         x_t = keep.tile([P, MODELS * TOKENS], BF16)
-        e_codes = keep.tile([P, MODELS * TOKENS], U32, align_bytes=64)
-        e_scales = keep.tile([P, MODELS * TOKENS], U8, align_bytes=64)
+        e_codes = keep.tile([P, MODELS, TOKENS], U32, align_bytes=64)
+        e_scales = keep.tile([P, MODELS, TOKENS], U8, align_bytes=64)
+        w1_codes = keep.tile([P, MODELS, D], I32, align_bytes=64)
+        w1_scales = keep.tile([P, 2, D], U8, align_bytes=64)
 
-        bias_col = keep.tile([P, 64], BF16)
-
-        def transpose_bias_rows():
-            bias_col_ps = psum_s.tile([P, P], BF16, tag="s")
-            nc.tensor.transpose(out=bias_col_ps[:], in_=bias_rows[:], identity=ident_bf[:])
-            nc.scalar.copy(out=bias_col[:], in_=bias_col_ps[:, 0:64])
-
-        def broadcast_biases(s):
-            layers = [layer for layer in range(2) if 0 <= s - 2 * layer < MODELS]
-            bias_ps = psum_s.tile([P, 2, D], BF16, tag="s")
-            for layer in layers:
-                for c in range(D // P):
-                    r = 32 * layer + 4 * (s - 2 * layer) + c
-                    nc.tensor.transpose(
-                        out=bias_ps[:, layer, P * c : P * (c + 1)],
-                        in_=bias_col[:, r : r + 1].to_broadcast([P, P]),
-                        identity=ident_bf[:],
-                    )
-            step_biases = sums.tile([P, 2, D], BF16)
-            written = slice(layers[0], layers[-1] + 1)
-            nc.scalar.copy(out=step_biases[:, written, :], in_=bias_ps[:, written, :])
-            return step_biases
+        emb_w_sorted = keep.tile([P, PACK, P], BF16)
+        rows_sorted = keep.tile([P, PACK, P], BF16)
+        col_t = keep.tile([P, PACK, EMB_B_ROW + 1], F32)
+        col_c = keep.tile([P, PACK, MODELS], BF16)
 
         def transpose_x(pair):
-            x_t_ps = psum_s.tile([P, 2 * PATCHES, P], BF16, tag="s")
+            x_t_ps = psum_e.tile([P, 2 * PATCHES, P], BF16, tag="e")
             for m in range(2):
                 for l in range(PATCHES):
                     n = 2 * pair + m
                     nc.tensor.transpose(
-                        out=x_t_ps[:, PATCHES * m + l, :], in_=x_sb[:, l, P * n : P * (n + 1)], identity=ident_bf[:]
+                        out=x_t_ps[:, PATCHES * m + l, :], in_=x_sb[:, l, P * n : P * (n + 1)], identity=ident[:]
                     )
             nc.scalar.copy(
                 out=x_t[:, 2 * TOKENS * pair : 2 * TOKENS * (pair + 1)], in_=x_t_ps[:].rearrange("s a b -> s (a b)")
             )
 
-        def embed_by_token(n):
+        def transpose_rows_by_t():
+            ps = psum_b.tile([P, PACK, P], BF16, tag="b")
+            for t in range(PACK):
+                nc.tensor.transpose(out=ps[:, t, :], in_=rows_sorted[:, t, :], identity=ident[:])
+            nc.vector.tensor_copy(out=col_t[:], in_=ps[:, :, 0 : EMB_B_ROW + 1])
+
+        def transpose_rows_by_c():
+            ps = psum_b.tile([P, PACK, P], BF16, tag="b")
+            for c in range(PACK):
+                nc.tensor.transpose(out=ps[:, c, :], in_=rows[:, P * c : P * (c + 1)], identity=ident[:])
+            nc.scalar.copy(out=col_c[:], in_=ps[:, :, B2_ROW : B2_ROW + MODELS])
+
+        def spread_b2(n):
+            ps = psum_b.tile([P, D], BF16, tag="b")
+            for c in range(PACK):
+                nc.tensor.transpose(
+                    out=ps[:, P * c : P * (c + 1)], in_=col_c[:, c, n : n + 1].to_broadcast([P, P]), identity=ident[:]
+                )
+            return ps
+
+        def b2_from_psum(ps):
+            b2 = stage.tile([P, D], BF16)
+            nc.scalar.copy(out=b2[:], in_=ps[:])
+            return b2
+
+        def embed(n):
+            with_bias = n in SCALAR_EMBEDS
             banks = []
             for l in range(PATCHES):
-                e_ps = psum_v.tile([P, PACK, P], F32, tag="v")
+                e_ps = psum_e.tile([P, PACK, P], F32, tag="e")
                 first = TOKENS * n + P * l
                 for t in range(PACK):
+                    if with_bias:
+                        nc.tensor.matmul(out=e_ps[:, t, :], lhsT=rows_sorted[:, t, :], rhs=pick[:], start=True, stop=False)
                     nc.tensor.matmul(
                         out=e_ps[:, t, :],
                         lhsT=emb_w_sorted[:, t, :],
                         rhs=x_t[:, first : first + P],
-                        start=True,
+                        start=not with_bias,
                         stop=True,
                     )
                 banks.append(e_ps)
             return banks
 
-        def words_from_psum(banks):
-            e_words = sums.tile([P, TOKENS, PACK], BF16, align_bytes=64)
+        def words_of(n, banks):
+            on_scalar = n in SCALAR_EMBEDS
+            e_words = stage.tile([P, TOKENS, PACK], BF16, align_bytes=64)
             for l in range(PATCHES):
-                nc.vector.tensor_tensor(
-                    out=e_words[:, P * l : P * (l + 1), :],
-                    in0=banks[l][:].rearrange("p t w -> p w t"),
-                    in1=emb_b_col[:].unsqueeze(1).to_broadcast([P, P, PACK]),
-                    op=ADD,
-                )
+                part = e_words[:, P * l : P * (l + 1), :]
+                by_token = banks[l][:].rearrange("p t w -> p w t")
+                if on_scalar:
+                    nc.scalar.copy(out=part, in_=by_token)
+                else:
+                    nc.vector.tensor_tensor(
+                        out=part,
+                        in0=by_token,
+                        in1=col_t[:, :, EMB_B_ROW].unsqueeze(1).to_broadcast([P, P, PACK]),
+                        op=ADD,
+                    )
             return e_words
-
-        def embed_planes(pair, first_t):
-            banks = []
-            for t in (first_t, first_t + 1):
-                e_ps = psum_s.tile([P, 2 * TOKENS], F32, tag="s")
-                nc.tensor.matmul(
-                    out=e_ps[:],
-                    lhsT=emb_w_sorted[:, t, :],
-                    rhs=x_t[:, 2 * TOKENS * pair : 2 * TOKENS * (pair + 1)],
-                    start=True,
-                    stop=True,
-                )
-                banks.append(e_ps)
-            return banks
-
-        def round_planes(e_planes, first_t, banks):
-            for i in range(2):
-                t = first_t + i
-                nc.scalar.activation(
-                    out=e_planes[:, t, :], in_=banks[i][:], func=IDENTITY, bias=emb_b_col[:, t : t + 1], scale=1.0
-                )
-
-        def words_from_planes(e_planes, m):
-            e_regrouped = stage.tile([P, TOKENS, PACK], BF16, align_bytes=64, bufs=1)
-            nc.gpsimd.tensor_scalar(
-                out=e_regrouped[:],
-                in0=e_planes[:, :, TOKENS * m : TOKENS * (m + 1)].rearrange("p t w -> p w t"),
-                scalar1=1.0,
-                scalar2=0.0,
-                op0=MULT,
-                op1=ADD,
-            )
-            return e_regrouped
 
         def quantise_embedding(n, e_words):
             nc.vector.quantize_mx(
-                out=e_codes[:, TOKENS * n : TOKENS * (n + 1)].bitcast(FP8X4),
-                scales=e_scales[:, TOKENS * n : TOKENS * (n + 1)],
-                in_=e_words[:].rearrange("p w t -> p (w t)"),
+                out=e_codes[:, n, :].bitcast(FP8X4), scales=e_scales[:, n, :], in_=e_words[:].rearrange("p w t -> p (w t)")
             )
 
-        def multiply(codes, scales, layer, n):
+        def sort_w1_codes(n):
+            nc.vector.tensor_copy(
+                out=w1_codes[:, n, :].rearrange("p (t c) -> p t c", t=PACK),
+                in_=words[:, 0, n, :].rearrange("p (c t) -> p t c", t=PACK),
+            )
+
+        def sort_w1_scales(half):
+            nc.vector.tensor_copy(
+                out=w1_scales[:, half, :].rearrange("p (t c) -> p c t", t=PACK),
+                in_=raw_scales[:, 0, half, :].rearrange("p (c t) -> p c t", t=PACK),
+            )
+
+        def first_product(n):
+            plane = 4 * (n % PLANES)
             banks = []
-            for l in range(PATCHES):
-                product = psum_v.tile([P, D], F32, tag="v")
-                nc.tensor.matmul_mx(
-                    out=product[:],
-                    lhsT=codes[:, P * l : P * (l + 1)].bitcast(FP8X4),
-                    lhsT_scale=scales[:, P * l : P * (l + 1)],
-                    rhs=w_words[:, layer, n, :].bitcast(FP8X4),
-                    rhs_scale=w_scales[:, layer, n, :],
-                    start=True,
-                    stop=True,
-                )
-                banks.append(product)
+            for pair in range(2):
+                a_ps = psum_a.tile([P, 2, TOKENS], F32, tag="a")
+                for i in range(2):
+                    cols = slice(P * (2 * pair + i), P * (2 * pair + i + 1))
+                    nc.tensor.matmul_mx(
+                        out=a_ps[:, i, :],
+                        lhsT=w1_codes[:, n, cols].bitcast(FP8X4),
+                        lhsT_scale=w1_scales[plane:P, n // PLANES, cols],
+                        rhs=e_codes[:, n, :].bitcast(FP8X4),
+                        rhs_scale=e_scales[:, n, :],
+                        start=True,
+                        stop=True,
+                    )
+                banks.append(a_ps)
             return banks
 
-        def add_b1(a_ps, step_biases):
-            a_sorted = sums.tile([P, PACK, P], F32)
-            nc.vector.tensor_tensor(
-                out=a_sorted[:],
-                in0=a_ps[:].rearrange("w (p t) -> w t p", t=PACK),
-                in1=step_biases[:, 0, :].rearrange("w (p t) -> w t p", t=PACK),
-                op=ADD,
-            )
-            return a_sorted
-
-        def gelu_transposed(a_sorted, g_words):
-            a_t_ps = psum_s.tile([P, PACK, P], F32, tag="s")
+        def gelu(n, banks):
+            g_planes = stage.tile([P, PACK, TOKENS], BF16)
             for t in range(PACK):
-                nc.tensor.transpose(out=a_t_ps[:, t, :], in_=a_sorted[:, t, :], identity=ident_f32[:])
-            nc.scalar.activation(out=g_words, in_=a_t_ps[:].rearrange("p t w -> p w t"), func=GELU)
+                nc.scalar.activation(
+                    out=g_planes[:, t, :], in_=banks[t // 2][:, t % 2, :], func=GELU, bias=col_t[:, t, n : n + 1], scale=1.0
+                )
+            return g_planes
 
-        def quantise_hidden(g_grouped):
+        def regroup(g_planes):
+            g_words = stage.tile([P, TOKENS, PACK], BF16, align_bytes=64)
+            by_token = g_planes[:].rearrange("p t w -> p w t")
+            nc.vector.tensor_copy(out=g_words[:], in_=by_token)
+            return g_words
+
+        def quantise_hidden(g_words):
             g_codes = stage.tile([P, TOKENS], U32, align_bytes=64)
             g_scales = stage.tile([P, TOKENS], U8, align_bytes=64)
             nc.vector.quantize_mx(
-                out=g_codes[:].bitcast(FP8X4),
-                scales=g_scales[:],
-                in_=g_grouped[:].rearrange("p l w t -> p (l w t)"),
+                out=g_codes[:].bitcast(FP8X4), scales=g_scales[:], in_=g_words[:].rearrange("p w t -> p (w t)")
             )
             return g_codes, g_scales
 
-        def add_b2_and_store(n, l, o_ps, step_biases):
-            o_sb = sums.tile([P, D], F32)
-            nc.vector.tensor_tensor(out=o_sb[:], in0=o_ps[:], in1=step_biases[:, 1, :], op=ADD)
+        def second_product(n, g_codes, g_scales):
+            plane = 4 * (n % PLANES)
+            banks = []
+            for l in range(PATCHES):
+                o_ps = psum_o.tile([P, D], F32, tag="o")
+                tokens = slice(P * l, P * (l + 1))
+                nc.tensor.matmul_mx(
+                    out=o_ps[:],
+                    lhsT=g_codes[:, tokens].bitcast(FP8X4),
+                    lhsT_scale=g_scales[:, tokens],
+                    rhs=words[:, 1, n, :].bitcast(FP8X4),
+                    rhs_scale=raw_scales[plane:P, 1, n // PLANES, :],
+                    start=True,
+                    stop=True,
+                )
+                banks.append(o_ps)
+            return banks
+
+        def add_b2_and_store(n, l, o_ps, b2):
+            o_sb = stage.tile([P, D], F32, bufs=4)
+            nc.vector.tensor_tensor(out=o_sb[:], in0=o_ps[:], in1=b2[:], op=ADD)
             nc.sync.dma_start(out=out[n, :, :, l, :].rearrange("b c d -> (b c) d"), in_=o_sb[:])
 
-        def first_product(n):
-            tokens = slice(TOKENS * n, TOKENS * (n + 1))
-            return multiply(e_codes[:, tokens], e_scales[:, tokens], 0, n)
+        e_banks, e_words, a_banks, g_planes, g_words, o_banks, b2 = {}, {}, {}, {}, {}, {}, {}
 
-        biases = {}
-        planes = {}
-        plane_banks = {}
-        e_words = {}
-        a_banks = {}
-        g_grouped = {}
-        o_banks = {}
-
+        nc.vector.tensor_copy(out=emb_w_sorted[:], in_=emb_w_sb[:].rearrange("s (p t) -> s t p", t=PACK))
         transpose_x(0)
-        transpose_x(1)
-        transpose_bias_rows()
-        e_words[0] = words_from_psum(embed_by_token(0))
-        quantise_embedding(0, e_words[0])
-        e_words[1] = words_from_psum(embed_by_token(1))
-        transpose_x(2)
-        transpose_x(3)
-        biases[0] = broadcast_biases(0)
-        planes[1] = stage.tile([P, PACK, 2 * TOKENS], BF16, name="e_planes", tag="e_planes")
-        round_planes(planes[1], 0, embed_planes(1, 0))
-        a_banks[0] = first_product(0)
-        round_planes(planes[1], 2, embed_planes(1, 2))
-        e_words[2] = words_from_planes(planes[1], 0)
-        biases[1] = broadcast_biases(1)
+        nc.vector.tensor_copy(out=rows_sorted[:], in_=rows[:].rearrange("r (p t) -> r t p", t=PACK))
+        e_banks[0] = embed(0)
+        transpose_rows_by_t()
+        b2_bank = None
 
-        for s in range(STEPS):
-            pair = (s - 1) // 2 + 2
-            if s >= 1 and pair < PAIRS:
-                round_planes(planes[pair], 2 * ((s - 1) % 2), plane_banks[s - 1])
-            if s < MODELS:
-                g_grouped[s] = stage.tile([P, PATCHES, P, PACK], BF16, name="g_grouped", tag="g_grouped", align_bytes=64)
-                gelu_transposed(add_b1(a_banks[s][0], biases[s]), g_grouped[s][:, 0])
-                a_sorted = add_b1(a_banks[s][1], biases[s])
-            if 1 <= s <= MODELS:
-                g_codes, g_scales = quantise_hidden(g_grouped[s - 1])
-            if s + 1 < MODELS:
-                quantise_embedding(s + 1, e_words[s + 1])
-            if 3 <= s + 2 < MODELS:
-                e_words[s + 2] = words_from_planes(planes[(s + 2) // 2], (s + 2) % 2)
-            if s + 2 < STEPS:
-                biases[s + 2] = broadcast_biases(s + 2)
-            if s < MODELS:
-                gelu_transposed(a_sorted, g_grouped[s][:, 1])
-            if s + 1 < MODELS:
+        for s in range(-2, MODELS + 1):
+            if 0 <= s + 1 < MODELS:
                 a_banks[s + 1] = first_product(s + 1)
-            if 1 <= s <= MODELS:
-                o_banks[s - 1] = multiply(g_codes, g_scales, 1, s - 1)
-            if s >= 2:
+            if s + 2 < MODELS and s + 2 in SCALAR_EMBEDS:
+                e_words[s + 2] = words_of(s + 2, e_banks[s + 2])
+            if 0 <= s < MODELS:
+                b2[s] = b2_from_psum(b2_bank)
+            if 0 <= s < MODELS:
+                g_words[s] = regroup(g_planes[s])
+            if s >= 1:
                 for l in range(PATCHES):
-                    add_b2_and_store(s - 2, l, o_banks[s - 2][l], biases[s])
-            pair = s // 2 + 2
-            if pair < PAIRS:
-                if s % 2 == 0:
-                    planes[pair] = stage.tile([P, PACK, 2 * TOKENS], BF16, name="e_planes", tag="e_planes")
-                plane_banks[s] = embed_planes(pair, 2 * (s % 2))
+                    add_b2_and_store(s - 1, l, o_banks[s - 1][l], b2[s - 1])
+            if 0 <= s + 1 < MODELS:
+                g_planes[s + 1] = gelu(s + 1, a_banks[s + 1])
+            if 0 <= s < MODELS:
+                g_codes = quantise_hidden(g_words[s])
+            if s % 2 == 0 and s // 2 + 2 < MODELS // 2:
+                transpose_x(s // 2 + 2)
+            if s + 3 < MODELS:
+                e_banks[s + 3] = embed(s + 3)
+            if s == -2:
+                transpose_rows_by_c()
+            if 0 <= s + 1 < MODELS:
+                b2_bank = spread_b2(s + 1)
+            if 0 <= s < MODELS:
+                o_banks[s] = second_product(s, *g_codes)
+            if s + 2 < MODELS and s + 2 not in SCALAR_EMBEDS:
+                e_words[s + 2] = words_of(s + 2, e_banks[s + 2])
+            if s == -2:
+                sort_w1_scales(0)
+            if s == 1:
+                sort_w1_scales(1)
+            if s + 2 < MODELS:
+                sort_w1_codes(s + 2)
+                quantise_embedding(s + 2, e_words[s + 2])

@@ -10,6 +10,7 @@ U32 = mybir.dt.uint32
 U8 = mybir.dt.uint8
 FP8X4 = mybir.dt.float8_e4m3fn_x4
 ADD = mybir.AluOpType.add
+MULT = mybir.AluOpType.mult
 GELU = mybir.ActivationFunctionType.Gelu_apprx_tanh
 
 P = 128
@@ -20,9 +21,9 @@ PATCHES = 2
 TOKENS = P * PATCHES
 QUADRANTS = 4
 PLANES = 4
-B1_ROW, EMB_B_ROW, B2_ROW = 0, 32, 64
 
-SCALAR_EMBEDS = (4, 5, 6, 7,)
+VECTOR_EMBEDS = ((0, 0), (0, 1))
+GPSIMD_SCALES = (0,)
 
 FLOPS = 2 * MODELS * TOKENS * (P * D + 2 * D * D)
 
@@ -35,20 +36,16 @@ def tile_model_pa_e_kernel(
         ctx.enter_context(tc.manual_schedule())
         keep = ctx.enter_context(tc.tile_pool(name="keep", bufs=1))
         stage = ctx.enter_context(tc.tile_pool(name="stage", bufs=3))
-        psum_a = ctx.enter_context(tc.psum_pool(name="psum_a", bufs=3))
+        psum_a = ctx.enter_context(tc.psum_pool(name="psum_a", bufs=4))
         psum_o = ctx.enter_context(tc.psum_pool(name="psum_o", bufs=2))
         psum_e = ctx.enter_context(tc.psum_pool(name="psum_e", bufs=2))
-        psum_b = ctx.enter_context(tc.psum_pool(name="psum_b", bufs=1))
 
+        raw_scales = keep.tile([P, 2, 2, D], U8, align_bytes=64)
+        nc.vector.memset(raw_scales[:].rearrange("p w g c -> p (w g c)").bitcast(I32), 0)
         warm = keep.tile([P, 1], F32)
         nc.vector.memset(warm[:], 0.0)
         rows = keep.tile([P, D], BF16)
         nc.vector.memset(rows[:], 0.0)
-        raw_scales = keep.tile([P, 2, 2, D], U8, align_bytes=64)
-        nc.vector.memset(raw_scales[:].rearrange("p w g c -> p (w g c)").bitcast(I32), 0)
-        pick = keep.tile([P, P], BF16)
-        nc.vector.memset(pick[:], 0.0)
-        nc.vector.memset(pick[EMB_B_ROW : EMB_B_ROW + 1, :], 1.0)
 
         words = keep.tile([P, 2, MODELS, D], I32, align_bytes=64)
 
@@ -67,20 +64,24 @@ def tile_model_pa_e_kernel(
 
         x_sb = keep.tile([P, PATCHES, MODELS * P], BF16)
         x_rows = x.rearrange("b c (l t) -> (b c) l t", l=PATCHES)
-        nc.sync.dma_start(out=x_sb[:, :, 0 : 2 * P], in_=x_rows[:, :, 0 : 2 * P])
+        half = MODELS // 2 * P
+        nc.sync.dma_start(out=x_sb[:, :, 0:half], in_=x_rows[:, :, 0:half])
         emb_w_sb = keep.tile([P, D], BF16)
         nc.sync.dma_start(out=emb_w_sb[:], in_=emb_W)
-        nc.scalar.dma_start(out=rows[EMB_B_ROW : EMB_B_ROW + 1, :], in_=emb_b.rearrange("(o d) -> o d", o=1))
-        nc.scalar.dma_start(out=rows[B1_ROW : B1_ROW + MODELS, :], in_=enc_b1)
-        nc.scalar.dma_start(out=rows[B2_ROW : B2_ROW + MODELS, :], in_=enc_b2)
-        nc.sync.dma_start(out=x_sb[:, :, 2 * P : 4 * P], in_=x_rows[:, :, 2 * P : 4 * P])
+        emb_b_col_bf = keep.tile([P, PACK], BF16)
+        nc.scalar.dma_start(out=emb_b_col_bf[:], in_=emb_b.rearrange("(p t) -> p t", t=PACK))
+        emb_b_bf = keep.tile([P, D], BF16)
+        nc.scalar.dma_start(out=emb_b_bf[:], in_=emb_b.partition_broadcast(P))
         load_scales(0, enc_W1_scales, 0)
         load_words(0, enc_W1_words, 0)
+        nc.sync.dma_start(out=rows[0:MODELS, :], in_=enc_b1)
         load_words(0, enc_W1_words, 1)
-        nc.sync.dma_start(out=x_sb[:, :, 4 * P :], in_=x_rows[:, :, 4 * P :])
         load_scales(1, enc_W2_scales, 0)
         load_words(1, enc_W2_words, 0)
+        nc.sync.dma_start(out=x_sb[:, :, half:], in_=x_rows[:, :, half:])
         load_words(0, enc_W1_words, 2)
+        b2 = keep.tile([P, MODELS, D], BF16)
+        nc.sync.dma_start(out=b2[:].rearrange("p n d -> p (n d)"), in_=enc_b2.rearrange("n d -> (n d)").partition_broadcast(P))
         load_words(1, enc_W2_words, 1)
         load_words(0, enc_W1_words, 3)
         load_scales(0, enc_W1_scales, 1)
@@ -94,6 +95,8 @@ def tile_model_pa_e_kernel(
         nc.scalar.activation(out=warm[:], in_=warm[:], func=GELU)
         ident = keep.tile([P, P], BF16)
         make_identity(nc, ident[:])
+        ident_f32 = keep.tile([P, P], F32)
+        make_identity(nc, ident_f32[:])
 
         x_t = keep.tile([P, MODELS * TOKENS], BF16)
         e_codes = keep.tile([P, MODELS, TOKENS], U32, align_bytes=64)
@@ -101,10 +104,19 @@ def tile_model_pa_e_kernel(
         w1_codes = keep.tile([P, MODELS, D], I32, align_bytes=64)
         w1_scales = keep.tile([P, 2, D], U8, align_bytes=64)
 
+        emb_b_rows = keep.tile([P, PACK, P], F32)
+        nc.gpsimd.tensor_scalar(
+            out=emb_b_rows[:],
+            in0=emb_b_bf[:].rearrange("w (p t) -> w t p", t=PACK),
+            scalar1=1.0,
+            scalar2=0.0,
+            op0=MULT,
+            op1=ADD,
+        )
         emb_w_sorted = keep.tile([P, PACK, P], BF16)
         rows_sorted = keep.tile([P, PACK, P], BF16)
-        col_t = keep.tile([P, PACK, EMB_B_ROW + 1], F32)
-        col_c = keep.tile([P, PACK, MODELS], BF16)
+        emb_b_col = keep.tile([P, PACK], F32)
+        b1_col = keep.tile([P, PACK, MODELS], F32)
 
         def transpose_x(pair):
             x_t_ps = psum_e.tile([P, 2 * PATCHES, P], BF16, tag="e")
@@ -119,64 +131,53 @@ def tile_model_pa_e_kernel(
             )
 
         def transpose_rows_by_t():
-            ps = psum_b.tile([P, PACK, P], BF16, tag="b")
+            ps = psum_e.tile([P, PACK, P], BF16, tag="e")
             for t in range(PACK):
                 nc.tensor.transpose(out=ps[:, t, :], in_=rows_sorted[:, t, :], identity=ident[:])
-            nc.vector.tensor_copy(out=col_t[:], in_=ps[:, :, 0 : EMB_B_ROW + 1])
+            nc.scalar.copy(out=b1_col[:], in_=ps[:, :, 0:MODELS])
 
-        def transpose_rows_by_c():
-            ps = psum_b.tile([P, PACK, P], BF16, tag="b")
-            for c in range(PACK):
-                nc.tensor.transpose(out=ps[:, c, :], in_=rows[:, P * c : P * (c + 1)], identity=ident[:])
-            nc.scalar.copy(out=col_c[:], in_=ps[:, :, B2_ROW : B2_ROW + MODELS])
-
-        def spread_b2(n):
-            ps = psum_b.tile([P, D], BF16, tag="b")
-            for c in range(PACK):
-                nc.tensor.transpose(
-                    out=ps[:, P * c : P * (c + 1)], in_=col_c[:, c, n : n + 1].to_broadcast([P, P]), identity=ident[:]
-                )
-            return ps
-
-        def b2_from_psum(ps):
-            b2 = stage.tile([P, D], BF16)
-            nc.scalar.copy(out=b2[:], in_=ps[:])
-            return b2
 
         def embed(n):
-            with_bias = n in SCALAR_EMBEDS
             banks = []
             for l in range(PATCHES):
-                e_ps = psum_e.tile([P, PACK, P], F32, tag="e")
+                pool, tag = (psum_o, "o") if n == 0 else (psum_e, "e")
+                e_ps = pool.tile([P, PACK, P], F32, name="e_ps", tag=tag)
                 first = TOKENS * n + P * l
+                seeded = (n, l) not in VECTOR_EMBEDS
                 for t in range(PACK):
-                    if with_bias:
-                        nc.tensor.matmul(out=e_ps[:, t, :], lhsT=rows_sorted[:, t, :], rhs=pick[:], start=True, stop=False)
+                    if seeded:
+                        nc.tensor.matmul(
+                            out=e_ps[:, t, :],
+                            lhsT=emb_b_rows[:, t, :],
+                            rhs=ident_f32[:],
+                            start=True,
+                            stop=False,
+                            is_transpose=True,
+                        )
                     nc.tensor.matmul(
                         out=e_ps[:, t, :],
                         lhsT=emb_w_sorted[:, t, :],
                         rhs=x_t[:, first : first + P],
-                        start=not with_bias,
+                        start=not seeded,
                         stop=True,
                     )
                 banks.append(e_ps)
             return banks
 
         def words_of(n, banks):
-            on_scalar = n in SCALAR_EMBEDS
             e_words = stage.tile([P, TOKENS, PACK], BF16, align_bytes=64)
             for l in range(PATCHES):
                 part = e_words[:, P * l : P * (l + 1), :]
                 by_token = banks[l][:].rearrange("p t w -> p w t")
-                if on_scalar:
-                    nc.scalar.copy(out=part, in_=by_token)
-                else:
+                if (n, l) in VECTOR_EMBEDS:
                     nc.vector.tensor_tensor(
                         out=part,
                         in0=by_token,
-                        in1=col_t[:, :, EMB_B_ROW].unsqueeze(1).to_broadcast([P, P, PACK]),
+                        in1=emb_b_col[:].unsqueeze(1).to_broadcast([P, P, PACK]),
                         op=ADD,
                     )
+                else:
+                    nc.scalar.copy(out=part, in_=by_token)
             return e_words
 
         def quantise_embedding(n, e_words):
@@ -191,7 +192,7 @@ def tile_model_pa_e_kernel(
             )
 
         def sort_w1_scales(half):
-            nc.vector.tensor_copy(
+            (nc.gpsimd if half in GPSIMD_SCALES else nc.vector).tensor_copy(
                 out=w1_scales[:, half, :].rearrange("p (t c) -> p c t", t=PACK),
                 in_=raw_scales[:, 0, half, :].rearrange("p (c t) -> p c t", t=PACK),
             )
@@ -219,7 +220,7 @@ def tile_model_pa_e_kernel(
             g_planes = stage.tile([P, PACK, TOKENS], BF16)
             for t in range(PACK):
                 nc.scalar.activation(
-                    out=g_planes[:, t, :], in_=banks[t // 2][:, t % 2, :], func=GELU, bias=col_t[:, t, n : n + 1], scale=1.0
+                    out=g_planes[:, t, :], in_=banks[t // 2][:, t % 2, :], func=GELU, bias=b1_col[:, t, n : n + 1], scale=1.0
                 )
             return g_planes
 
@@ -255,52 +256,50 @@ def tile_model_pa_e_kernel(
                 banks.append(o_ps)
             return banks
 
-        def add_b2_and_store(n, l, o_ps, b2):
+        def add_b2_and_store(n, l, o_ps):
             o_sb = stage.tile([P, D], F32, bufs=4)
-            nc.vector.tensor_tensor(out=o_sb[:], in0=o_ps[:], in1=b2[:], op=ADD)
+            nc.vector.tensor_tensor(out=o_sb[:], in0=o_ps[:], in1=b2[:, n, :], op=ADD)
             nc.sync.dma_start(out=out[n, :, :, l, :].rearrange("b c d -> (b c) d"), in_=o_sb[:])
 
-        e_banks, e_words, a_banks, g_planes, g_words, o_banks, b2 = {}, {}, {}, {}, {}, {}, {}
+        e_banks, e_words, a_banks, g_planes, g_words, o_banks = {}, {}, {}, {}, {}, {}
 
         nc.vector.tensor_copy(out=emb_w_sorted[:], in_=emb_w_sb[:].rearrange("s (p t) -> s t p", t=PACK))
+        nc.vector.tensor_copy(out=emb_b_col[:], in_=emb_b_col_bf[:])
         transpose_x(0)
-        nc.vector.tensor_copy(out=rows_sorted[:], in_=rows[:].rearrange("r (p t) -> r t p", t=PACK))
+        transpose_x(1)
         e_banks[0] = embed(0)
-        transpose_rows_by_t()
-        b2_bank = None
+        e_banks[1] = embed(1)
 
-        for s in range(-2, MODELS + 1):
-            if 0 <= s + 1 < MODELS:
-                a_banks[s + 1] = first_product(s + 1)
-            if s + 2 < MODELS and s + 2 in SCALAR_EMBEDS:
-                e_words[s + 2] = words_of(s + 2, e_banks[s + 2])
-            if 0 <= s < MODELS:
-                b2[s] = b2_from_psum(b2_bank)
+        for s in range(-3, MODELS + 1):
             if 0 <= s < MODELS:
                 g_words[s] = regroup(g_planes[s])
             if s >= 1:
-                for l in range(PATCHES):
-                    add_b2_and_store(s - 1, l, o_banks[s - 1][l], b2[s - 1])
-            if 0 <= s + 1 < MODELS:
-                g_planes[s + 1] = gelu(s + 1, a_banks[s + 1])
+                add_b2_and_store(s - 1, 0, o_banks[s - 1][0])
             if 0 <= s < MODELS:
                 g_codes = quantise_hidden(g_words[s])
-            if s % 2 == 0 and s // 2 + 2 < MODELS // 2:
-                transpose_x(s // 2 + 2)
-            if s + 3 < MODELS:
-                e_banks[s + 3] = embed(s + 3)
-            if s == -2:
-                transpose_rows_by_c()
-            if 0 <= s + 1 < MODELS:
-                b2_bank = spread_b2(s + 1)
             if 0 <= s < MODELS:
                 o_banks[s] = second_product(s, *g_codes)
-            if s + 2 < MODELS and s + 2 not in SCALAR_EMBEDS:
-                e_words[s + 2] = words_of(s + 2, e_banks[s + 2])
-            if s == -2:
-                sort_w1_scales(0)
-            if s == 1:
-                sort_w1_scales(1)
-            if s + 2 < MODELS:
-                sort_w1_codes(s + 2)
+            if s >= 1:
+                add_b2_and_store(s - 1, 1, o_banks[s - 1][1])
+            if 0 <= s + 2 < MODELS:
                 quantise_embedding(s + 2, e_words[s + 2])
+            if 0 <= s + 2 < MODELS:
+                a_banks[s + 2] = first_product(s + 2)
+            if 0 <= s + 1 < MODELS:
+                g_planes[s + 1] = gelu(s + 1, a_banks[s + 1])
+            if s + 3 < MODELS and s != -2:
+                e_words[s + 3] = words_of(s + 3, e_banks[s + 3])
+            if s == -3:
+                e_words[1] = words_of(1, e_banks[1])
+                nc.vector.tensor_copy(out=rows_sorted[:], in_=rows[:].rearrange("r (p t) -> r t p", t=PACK))
+                transpose_rows_by_t()
+            if s in (-1, 1):
+                transpose_x(2 + (s + 1) // 2)
+            if 2 <= s + 4 < MODELS:
+                e_banks[s + 4] = embed(s + 4)
+            if s == -3:
+                sort_w1_scales(0)
+            if s == 0:
+                sort_w1_scales(1)
+            if s + 3 < MODELS:
+                sort_w1_codes(s + 3)

@@ -10,7 +10,6 @@ U32 = mybir.dt.uint32
 U8 = mybir.dt.uint8
 FP8X4 = mybir.dt.float8_e4m3fn_x4
 ADD = mybir.AluOpType.add
-MULT = mybir.AluOpType.mult
 GELU = mybir.ActivationFunctionType.Gelu_apprx_tanh
 
 P = 128
@@ -23,7 +22,6 @@ QUADRANTS = 4
 PLANES = 4
 
 VECTOR_EMBEDS = ((0, 0), (0, 1))
-GPSIMD_SCALES = (0,)
 
 FLOPS = 2 * MODELS * TOKENS * (P * D + 2 * D * D)
 
@@ -40,26 +38,45 @@ def tile_model_pa_e_kernel(
         psum_o = ctx.enter_context(tc.psum_pool(name="psum_o", bufs=2))
         psum_e = ctx.enter_context(tc.psum_pool(name="psum_e", bufs=2))
 
-        raw_scales = keep.tile([P, 2, 2, D], U8, align_bytes=64)
-        nc.vector.memset(raw_scales[:].rearrange("p w g c -> p (w g c)").bitcast(I32), 0)
-        warm = keep.tile([P, 1], F32)
-        nc.vector.memset(warm[:], 0.0)
         rows = keep.tile([P, D], BF16)
         nc.vector.memset(rows[:], 0.0)
+        raw_scales = keep.tile([P, 2, D], U8, align_bytes=64)
+        nc.vector.memset(raw_scales[:].rearrange("p g c -> p (g c)").bitcast(I32), 0)
+        w2_scales = keep.tile([P, MODELS, D], U8, align_bytes=64)
+        nc.vector.memset(w2_scales[:].rearrange("p n c -> p (n c)").bitcast(I32), 0)
+        warm = keep.tile([P, 1], F32)
+        nc.vector.memset(warm[:], 0.0)
 
         words = keep.tile([P, 2, MODELS, D], I32, align_bytes=64)
 
-        def load_scales(layer, scales, half):
+        def load_w1_scales(half):
             first = PLANES * half
             for q in range(QUADRANTS):
                 nc.sync.dma_start(
-                    out=raw_scales[32 * q : 32 * q + 4 * PLANES, layer, half, :].bitcast(I32),
-                    in_=scales[first : first + PLANES, 4 * q : 4 * q + 4, :].bitcast(I32),
+                    out=raw_scales[32 * q : 32 * q + 4 * PLANES, half, :].bitcast(I32),
+                    in_=enc_W1_scales[first : first + PLANES, 4 * q : 4 * q + 4, :].bitcast(I32),
                 )
 
-        def load_words(layer, given, n):
+        def load_w2_scales():
+            for q in range(QUADRANTS):
+                nc.sync.dma_start(
+                    out=w2_scales[32 * q : 32 * q + 4, :, :].bitcast(I32),
+                    in_=enc_W2_scales.bitcast(I32)[:, 4 * q : 4 * q + 4, :].rearrange("g r c -> r g c"),
+                )
+
+        def load_words(layer, first, last):
+            given = (enc_W1_words, enc_W2_words)[layer]
             nc.sync.dma_start(
-                out=words[:, layer, n, :], in_=given[n].rearrange("p c t -> p (c t)").bitcast(I32)
+                out=words[:, layer, first : last + 1, :],
+                in_=given[first : last + 1].rearrange("g p c t -> p g (c t)").bitcast(I32),
+            )
+
+        b2 = keep.tile([P, MODELS, D], BF16)
+
+        def load_b2(first, last):
+            nc.sync.dma_start(
+                out=b2[:, first : last + 1, :].rearrange("p n d -> p (n d)"),
+                in_=enc_b2[first : last + 1, :].rearrange("n d -> (n d)").partition_broadcast(P),
             )
 
         x_sb = keep.tile([P, PATCHES, MODELS * P], BF16)
@@ -70,27 +87,17 @@ def tile_model_pa_e_kernel(
         nc.sync.dma_start(out=emb_w_sb[:], in_=emb_W)
         emb_b_col_bf = keep.tile([P, PACK], BF16)
         nc.scalar.dma_start(out=emb_b_col_bf[:], in_=emb_b.rearrange("(p t) -> p t", t=PACK))
-        emb_b_bf = keep.tile([P, D], BF16)
-        nc.scalar.dma_start(out=emb_b_bf[:], in_=emb_b.partition_broadcast(P))
-        load_scales(0, enc_W1_scales, 0)
-        load_words(0, enc_W1_words, 0)
-        nc.sync.dma_start(out=rows[0:MODELS, :], in_=enc_b1)
-        load_words(0, enc_W1_words, 1)
-        load_scales(1, enc_W2_scales, 0)
-        load_words(1, enc_W2_words, 0)
+        nc.scalar.dma_start(out=rows[0:MODELS, :], in_=enc_b1)
+        load_w1_scales(0)
+        load_words(0, 0, 0)
+        load_words(0, 1, 1)
+        load_w2_scales()
+        load_words(1, 0, 0)
         nc.sync.dma_start(out=x_sb[:, :, half:], in_=x_rows[:, :, half:])
-        load_words(0, enc_W1_words, 2)
-        b2 = keep.tile([P, MODELS, D], BF16)
-        nc.sync.dma_start(out=b2[:].rearrange("p n d -> p (n d)"), in_=enc_b2.rearrange("n d -> (n d)").partition_broadcast(P))
-        load_words(1, enc_W2_words, 1)
-        load_words(0, enc_W1_words, 3)
-        load_scales(0, enc_W1_scales, 1)
-        load_scales(1, enc_W2_scales, 1)
-        load_words(1, enc_W2_words, 2)
-        for n in range(4, MODELS):
-            load_words(0, enc_W1_words, n)
-            load_words(1, enc_W2_words, n - 1)
-        load_words(1, enc_W2_words, MODELS - 1)
+        load_words(0, 2, 3)
+        load_b2(0, 3)
+        load_words(1, 1, 1)
+        load_w1_scales(1)
 
         nc.scalar.activation(out=warm[:], in_=warm[:], func=GELU)
         ident = keep.tile([P, P], BF16)
@@ -105,14 +112,6 @@ def tile_model_pa_e_kernel(
         w1_scales = keep.tile([P, 2, D], U8, align_bytes=64)
 
         emb_b_rows = keep.tile([P, PACK, P], F32)
-        nc.gpsimd.tensor_scalar(
-            out=emb_b_rows[:],
-            in0=emb_b_bf[:].rearrange("w (p t) -> w t p", t=PACK),
-            scalar1=1.0,
-            scalar2=0.0,
-            op0=MULT,
-            op1=ADD,
-        )
         emb_w_sorted = keep.tile([P, PACK, P], BF16)
         rows_sorted = keep.tile([P, PACK, P], BF16)
         emb_b_col = keep.tile([P, PACK], F32)
@@ -130,8 +129,16 @@ def tile_model_pa_e_kernel(
                 out=x_t[:, 2 * TOKENS * pair : 2 * TOKENS * (pair + 1)], in_=x_t_ps[:].rearrange("s a b -> s (a b)")
             )
 
+        def spread_emb_b():
+            ps = psum_a.tile([P, PACK, P], F32, tag="a")
+            for t in range(PACK):
+                nc.tensor.transpose(
+                    out=ps[:, t, :], in_=emb_b_col[:, t : t + 1].to_broadcast([P, P]), identity=ident_f32[:]
+                )
+            nc.scalar.copy(out=emb_b_rows[:], in_=ps[:])
+
         def transpose_rows_by_t():
-            ps = psum_e.tile([P, PACK, P], BF16, tag="e")
+            ps = psum_a.tile([P, PACK, P], BF16, tag="a")
             for t in range(PACK):
                 nc.tensor.transpose(out=ps[:, t, :], in_=rows_sorted[:, t, :], identity=ident[:])
             nc.scalar.copy(out=b1_col[:], in_=ps[:, :, 0:MODELS])
@@ -192,9 +199,9 @@ def tile_model_pa_e_kernel(
             )
 
         def sort_w1_scales(half):
-            (nc.gpsimd if half in GPSIMD_SCALES else nc.vector).tensor_copy(
+            nc.vector.tensor_copy(
                 out=w1_scales[:, half, :].rearrange("p (t c) -> p c t", t=PACK),
-                in_=raw_scales[:, 0, half, :].rearrange("p (c t) -> p c t", t=PACK),
+                in_=raw_scales[:, half, :].rearrange("p (c t) -> p c t", t=PACK),
             )
 
         def first_product(n):
@@ -239,7 +246,6 @@ def tile_model_pa_e_kernel(
             return g_codes, g_scales
 
         def second_product(n, g_codes, g_scales):
-            plane = 4 * (n % PLANES)
             banks = []
             for l in range(PATCHES):
                 o_ps = psum_o.tile([P, D], F32, tag="o")
@@ -249,38 +255,59 @@ def tile_model_pa_e_kernel(
                     lhsT=g_codes[:, tokens].bitcast(FP8X4),
                     lhsT_scale=g_scales[:, tokens],
                     rhs=words[:, 1, n, :].bitcast(FP8X4),
-                    rhs_scale=raw_scales[plane:P, 1, n // PLANES, :],
+                    rhs_scale=w2_scales[:, n, :],
                     start=True,
                     stop=True,
                 )
                 banks.append(o_ps)
             return banks
 
-        def add_b2_and_store(n, l, o_ps):
-            o_sb = stage.tile([P, D], F32, bufs=4)
-            nc.vector.tensor_tensor(out=o_sb[:], in0=o_ps[:], in1=b2[:, n, :], op=ADD)
-            nc.sync.dma_start(out=out[n, :, :, l, :].rearrange("b c d -> (b c) d"), in_=o_sb[:])
+        def add_b2(n, l, o_ps, o_sb):
+            nc.vector.tensor_tensor(out=o_sb[:, l, :], in0=o_ps[:], in1=b2[:, n, :], op=ADD)
 
-        e_banks, e_words, a_banks, g_planes, g_words, o_banks = {}, {}, {}, {}, {}, {}
+        def store(n, first, last):
+            nc.sync.dma_start(
+                out=out[n, :, :, first : last + 1, :].rearrange("b c l d -> (b c) l d"), in_=o_sb[n][:, first : last + 1, :]
+            )
+
+
+        e_banks, e_words, a_banks, g_planes, g_words, o_banks, o_sb = {}, {}, {}, {}, {}, {}, {}
 
         nc.vector.tensor_copy(out=emb_w_sorted[:], in_=emb_w_sb[:].rearrange("s (p t) -> s t p", t=PACK))
         nc.vector.tensor_copy(out=emb_b_col[:], in_=emb_b_col_bf[:])
         transpose_x(0)
         transpose_x(1)
         e_banks[0] = embed(0)
+        spread_emb_b()
         e_banks[1] = embed(1)
-
         for s in range(-3, MODELS + 1):
+            if s == -1:
+                load_words(0, 4, 5)
+                load_words(1, 2, 3)
+            if s == 0:
+                load_b2(4, 7)
+            if s == 1:
+                load_words(0, 6, 7)
+                load_words(1, 4, 5)
+            if s == 3:
+                load_words(1, 6, 7)
             if 0 <= s < MODELS:
                 g_words[s] = regroup(g_planes[s])
             if s >= 1:
-                add_b2_and_store(s - 1, 0, o_banks[s - 1][0])
+                o_sb[s - 1] = stage.tile([P, PATCHES, D], F32, name="o_sb", tag="o_sb", bufs=MODELS)
+                add_b2(s - 1, 0, o_banks[s - 1][0], o_sb[s - 1])
+                if s == MODELS:
+                    store(s - 1, 0, 0)
             if 0 <= s < MODELS:
                 g_codes = quantise_hidden(g_words[s])
             if 0 <= s < MODELS:
                 o_banks[s] = second_product(s, *g_codes)
             if s >= 1:
-                add_b2_and_store(s - 1, 1, o_banks[s - 1][1])
+                add_b2(s - 1, 1, o_banks[s - 1][1], o_sb[s - 1])
+                if s < MODELS:
+                    store(s - 1, 0, 1)
+                else:
+                    store(s - 1, 1, 1)
             if 0 <= s + 2 < MODELS:
                 quantise_embedding(s + 2, e_words[s + 2])
             if 0 <= s + 2 < MODELS:
@@ -291,15 +318,16 @@ def tile_model_pa_e_kernel(
                 e_words[s + 3] = words_of(s + 3, e_banks[s + 3])
             if s == -3:
                 e_words[1] = words_of(1, e_banks[1])
-                nc.vector.tensor_copy(out=rows_sorted[:], in_=rows[:].rearrange("r (p t) -> r t p", t=PACK))
-                transpose_rows_by_t()
             if s in (-1, 1):
                 transpose_x(2 + (s + 1) // 2)
             if 2 <= s + 4 < MODELS:
                 e_banks[s + 4] = embed(s + 4)
             if s == -3:
                 sort_w1_scales(0)
-            if s == 0:
+            if s == 1:
                 sort_w1_scales(1)
             if s + 3 < MODELS:
                 sort_w1_codes(s + 3)
+            if s == -3:
+                nc.vector.tensor_copy(out=rows_sorted[:], in_=rows[:].rearrange("r (p t) -> r t p", t=PACK))
+                transpose_rows_by_t()

@@ -151,22 +151,23 @@ def tile_model_pa_e_kernel(
                 e_ps = pool.tile([P, PACK, P], F32, name="e_ps", tag=tag)
                 first = TOKENS * n + P * l
                 seeded = (n, l) not in VECTOR_EMBEDS
-                for t in range(PACK):
-                    if seeded:
+                if seeded:
+                    for t in range(PACK):
                         nc.tensor.matmul(
                             out=e_ps[:, t, :],
                             lhsT=emb_b_rows[:, t, :],
                             rhs=ident_f32[:],
-                            start=True,
+                            start=t == 0,
                             stop=False,
                             is_transpose=True,
                         )
+                for t in range(PACK):
                     nc.tensor.matmul(
                         out=e_ps[:, t, :],
                         lhsT=emb_w_sorted[:, t, :],
                         rhs=x_t[:, first : first + P],
                         start=not seeded,
-                        stop=True,
+                        stop=not seeded or t == PACK - 1,
                     )
                 banks.append(e_ps)
             return banks

@@ -22,6 +22,7 @@ QUADRANTS = 4
 PLANES = 4
 
 VECTOR_EMBEDS = ((0, 0), (0, 1))
+CHUNK = 4
 
 FLOPS = 2 * MODELS * TOKENS * (P * D + 2 * D * D)
 
@@ -145,31 +146,30 @@ def tile_model_pa_e_kernel(
 
 
         def embed(n):
-            banks = []
+            pool, tag = (psum_o, "o") if n == 0 else (psum_e, "e")
+            banks = [pool.tile([P, PACK, P], F32, name="e_ps", tag=tag) for l in range(PATCHES)]
+            seeded = [(n, l) not in VECTOR_EMBEDS for l in range(PATCHES)]
             for l in range(PATCHES):
-                pool, tag = (psum_o, "o") if n == 0 else (psum_e, "e")
-                e_ps = pool.tile([P, PACK, P], F32, name="e_ps", tag=tag)
-                first = TOKENS * n + P * l
-                seeded = (n, l) not in VECTOR_EMBEDS
-                if seeded:
+                if seeded[l]:
                     for t in range(PACK):
                         nc.tensor.matmul(
-                            out=e_ps[:, t, :],
+                            out=banks[l][:, t, :],
                             lhsT=emb_b_rows[:, t, :],
                             rhs=ident_f32[:],
                             start=t == 0,
                             stop=False,
                             is_transpose=True,
                         )
+            for l in range(PATCHES):
+                first = TOKENS * n + P * l
                 for t in range(PACK):
                     nc.tensor.matmul(
-                        out=e_ps[:, t, :],
+                        out=banks[l][:, t, :],
                         lhsT=emb_w_sorted[:, t, :],
                         rhs=x_t[:, first : first + P],
-                        start=not seeded,
-                        stop=not seeded or t == PACK - 1,
+                        start=not seeded[l],
+                        stop=not seeded[l] or t == PACK - 1,
                     )
-                banks.append(e_ps)
             return banks
 
         def words_of(n, banks):
@@ -234,8 +234,10 @@ def tile_model_pa_e_kernel(
 
         def regroup(g_planes):
             g_words = stage.tile([P, TOKENS, PACK], BF16, align_bytes=64)
-            by_token = g_planes[:].rearrange("p t w -> p w t")
-            nc.vector.tensor_copy(out=g_words[:], in_=by_token)
+            nc.vector.tensor_copy(
+                out=g_words[:].rearrange("p (c i) t -> p c t i", i=CHUNK),
+                in_=g_planes[:].rearrange("p t (c i) -> p c t i", i=CHUNK),
+            )
             return g_words
 
         def quantise_hidden(g_words):
@@ -277,9 +279,9 @@ def tile_model_pa_e_kernel(
         nc.vector.tensor_copy(out=emb_w_sorted[:], in_=emb_w_sb[:].rearrange("s (p t) -> s t p", t=PACK))
         nc.vector.tensor_copy(out=emb_b_col[:], in_=emb_b_col_bf[:])
         transpose_x(0)
-        transpose_x(1)
-        e_banks[0] = embed(0)
         spread_emb_b()
+        e_banks[0] = embed(0)
+        transpose_x(1)
         e_banks[1] = embed(1)
         for s in range(-3, MODELS + 1):
             if s == -1:

@@ -23,6 +23,7 @@ PLANES = 4
 
 VECTOR_EMBEDS = ((0, 0), (0, 1))
 CHUNK = 4
+WARM_UPS = 4
 
 FLOPS = 2 * MODELS * TOKENS * (P * D + 2 * D * D)
 
@@ -39,8 +40,10 @@ def tile_model_pa_e_kernel(
         psum_o = ctx.enter_context(tc.psum_pool(name="psum_o", bufs=2))
         psum_e = ctx.enter_context(tc.psum_pool(name="psum_e", bufs=2))
 
+        zeros = keep.tile([P, D], BF16)
+        nc.vector.memset(zeros[:].bitcast(I32), 0)
         rows = keep.tile([P, D], BF16)
-        nc.vector.memset(rows[:], 0.0)
+        nc.vector.memset(rows[:].bitcast(I32), 0)
         raw_scales = keep.tile([P, 2, D], U8, align_bytes=64)
         nc.vector.memset(raw_scales[:].rearrange("p g c -> p (g c)").bitcast(I32), 0)
         w2_scales = keep.tile([P, MODELS, D], U8, align_bytes=64)
@@ -92,13 +95,13 @@ def tile_model_pa_e_kernel(
         load_w1_scales(0)
         load_words(0, 0, 0)
         load_words(0, 1, 1)
-        load_w2_scales()
         load_words(1, 0, 0)
+        load_w2_scales()
         nc.sync.dma_start(out=x_sb[:, :, half:], in_=x_rows[:, :, half:])
         load_words(0, 2, 3)
+        load_w1_scales(1)
         load_b2(0, 3)
         load_words(1, 1, 1)
-        load_w1_scales(1)
 
         nc.scalar.activation(out=warm[:], in_=warm[:], func=GELU)
         ident = keep.tile([P, P], BF16)
@@ -106,6 +109,9 @@ def tile_model_pa_e_kernel(
         ident_f32 = keep.tile([P, P], F32)
         make_identity(nc, ident_f32[:])
 
+        warm_up = psum_a.tile([P, D], F32, name="warm_up", tag="a")
+        for i in range(WARM_UPS):
+            nc.tensor.matmul(out=warm_up[:], lhsT=zeros[:, 0:P], rhs=zeros[:], start=True, stop=True)
         x_t = keep.tile([P, MODELS * TOKENS], BF16)
         e_codes = keep.tile([P, MODELS, TOKENS], U32, align_bytes=64)
         e_scales = keep.tile([P, MODELS, TOKENS], U8, align_bytes=64)
@@ -114,7 +120,6 @@ def tile_model_pa_e_kernel(
 
         emb_b_rows = keep.tile([P, PACK, P], F32)
         emb_w_sorted = keep.tile([P, PACK, P], BF16)
-        rows_sorted = keep.tile([P, PACK, P], BF16)
         emb_b_col = keep.tile([P, PACK], F32)
         b1_col = keep.tile([P, PACK, MODELS], F32)
 
@@ -141,14 +146,28 @@ def tile_model_pa_e_kernel(
         def transpose_rows_by_t():
             ps = psum_a.tile([P, PACK, P], BF16, tag="a")
             for t in range(PACK):
-                nc.tensor.transpose(out=ps[:, t, :], in_=rows_sorted[:, t, :], identity=ident[:])
+                nc.tensor.transpose(out=ps[:, t, :], in_=rows[:].rearrange("r (p t) -> r t p", t=PACK)[:, t, :], identity=ident[:])
             nc.scalar.copy(out=b1_col[:], in_=ps[:, :, 0:MODELS])
 
+
+        def multiply_patches(n, l, bank, alone):
+            first = TOKENS * n + P * l
+            for t in range(PACK):
+                nc.tensor.matmul(
+                    out=bank[:, t, :],
+                    lhsT=emb_w_sorted[:, t, :],
+                    rhs=x_t[:, first : first + P],
+                    start=alone,
+                    stop=alone or t == PACK - 1,
+                )
 
         def embed(n):
             pool, tag = (psum_o, "o") if n == 0 else (psum_e, "e")
             banks = [pool.tile([P, PACK, P], F32, name="e_ps", tag=tag) for l in range(PATCHES)]
             seeded = [(n, l) not in VECTOR_EMBEDS for l in range(PATCHES)]
+            for l in range(PATCHES):
+                if not seeded[l]:
+                    multiply_patches(n, l, banks[l], True)
             for l in range(PATCHES):
                 if seeded[l]:
                     for t in range(PACK):
@@ -161,15 +180,8 @@ def tile_model_pa_e_kernel(
                             is_transpose=True,
                         )
             for l in range(PATCHES):
-                first = TOKENS * n + P * l
-                for t in range(PACK):
-                    nc.tensor.matmul(
-                        out=banks[l][:, t, :],
-                        lhsT=emb_w_sorted[:, t, :],
-                        rhs=x_t[:, first : first + P],
-                        start=not seeded[l],
-                        stop=not seeded[l] or t == PACK - 1,
-                    )
+                if seeded[l]:
+                    multiply_patches(n, l, banks[l], False)
             return banks
 
         def words_of(n, banks):
@@ -332,5 +344,4 @@ def tile_model_pa_e_kernel(
             if s + 3 < MODELS:
                 sort_w1_codes(s + 3)
             if s == -3:
-                nc.vector.tensor_copy(out=rows_sorted[:], in_=rows[:].rearrange("r (p t) -> r t p", t=PACK))
                 transpose_rows_by_t()

@@ -10,6 +10,7 @@ U32 = mybir.dt.uint32
 U8 = mybir.dt.uint8
 FP8X4 = mybir.dt.float8_e4m3fn_x4
 ADD = mybir.AluOpType.add
+MULT = mybir.AluOpType.mult
 GELU = mybir.ActivationFunctionType.Gelu_apprx_tanh
 
 P = 128
@@ -24,6 +25,7 @@ PLANES = 4
 VECTOR_EMBEDS = ((0, 0), (0, 1))
 CHUNK = 4
 WARM_UPS = 4
+GPSIMD_REGROUPS = (3, 4, 5, 6,)
 
 FLOPS = 2 * MODELS * TOKENS * (P * D + 2 * D * D)
 
@@ -86,22 +88,22 @@ def tile_model_pa_e_kernel(
         x_sb = keep.tile([P, PATCHES, MODELS * P], BF16)
         x_rows = x.rearrange("b c (l t) -> (b c) l t", l=PATCHES)
         half = MODELS // 2 * P
-        nc.sync.dma_start(out=x_sb[:, :, 0:half], in_=x_rows[:, :, 0:half])
         emb_w_sb = keep.tile([P, D], BF16)
-        nc.sync.dma_start(out=emb_w_sb[:], in_=emb_W)
         emb_b_col_bf = keep.tile([P, PACK], BF16)
+        nc.sync.dma_start(out=x_sb[:, :, 0:half], in_=x_rows[:, :, 0:half])
+        nc.sync.dma_start(out=emb_w_sb[:], in_=emb_W)
         nc.scalar.dma_start(out=emb_b_col_bf[:], in_=emb_b.rearrange("(p t) -> p t", t=PACK))
         nc.scalar.dma_start(out=rows[0:MODELS, :], in_=enc_b1)
         load_w1_scales(0)
         load_words(0, 0, 0)
         load_words(0, 1, 1)
-        load_words(1, 0, 0)
         load_w2_scales()
+        load_words(1, 0, 0)
         nc.sync.dma_start(out=x_sb[:, :, half:], in_=x_rows[:, :, half:])
         load_words(0, 2, 3)
-        load_w1_scales(1)
         load_b2(0, 3)
         load_words(1, 1, 1)
+        load_w1_scales(1)
 
         nc.scalar.activation(out=warm[:], in_=warm[:], func=GELU)
         ident = keep.tile([P, P], BF16)
@@ -244,12 +246,16 @@ def tile_model_pa_e_kernel(
                 )
             return g_planes
 
-        def regroup(g_planes):
+        def regroup(n, g_planes):
             g_words = stage.tile([P, TOKENS, PACK], BF16, align_bytes=64)
-            nc.vector.tensor_copy(
-                out=g_words[:].rearrange("p (c i) t -> p c t i", i=CHUNK),
-                in_=g_planes[:].rearrange("p t (c i) -> p c t i", i=CHUNK),
-            )
+            by_token = g_planes[:].rearrange("p t w -> p w t")
+            if n in GPSIMD_REGROUPS:
+                nc.gpsimd.tensor_scalar(out=g_words[:], in0=by_token, scalar1=1.0, scalar2=0.0, op0=MULT, op1=ADD)
+            else:
+                nc.vector.tensor_copy(
+                    out=g_words[:].rearrange("p (c i) t -> p c t i", i=CHUNK),
+                    in_=g_planes[:].rearrange("p t (c i) -> p c t i", i=CHUNK),
+                )
             return g_words
 
         def quantise_hidden(g_words):
@@ -295,7 +301,16 @@ def tile_model_pa_e_kernel(
         e_banks[0] = embed(0)
         transpose_x(1)
         e_banks[1] = embed(1)
-        for s in range(-3, MODELS + 1):
+        def finish(n):
+            o_sb[n] = stage.tile([P, PATCHES, D], F32, name="o_sb", tag="o_sb", bufs=MODELS)
+            for l in range(PATCHES):
+                add_b2(n, l, o_banks[n][l], o_sb[n])
+                if n == MODELS - 1:
+                    store(n, l, l)
+            if n < MODELS - 1:
+                store(n, 0, 1)
+
+        for s in range(-3, MODELS):
             if s == -1:
                 load_words(0, 4, 5)
                 load_words(1, 2, 3)
@@ -306,29 +321,22 @@ def tile_model_pa_e_kernel(
                 load_words(1, 4, 5)
             if s == 3:
                 load_words(1, 6, 7)
-            if 0 <= s < MODELS:
-                g_words[s] = regroup(g_planes[s])
-            if s >= 1:
-                o_sb[s - 1] = stage.tile([P, PATCHES, D], F32, name="o_sb", tag="o_sb", bufs=MODELS)
-                add_b2(s - 1, 0, o_banks[s - 1][0], o_sb[s - 1])
-                if s == MODELS:
-                    store(s - 1, 0, 0)
-            if 0 <= s < MODELS:
-                g_codes = quantise_hidden(g_words[s])
-            if 0 <= s < MODELS:
-                o_banks[s] = second_product(s, *g_codes)
-            if s >= 1:
-                add_b2(s - 1, 1, o_banks[s - 1][1], o_sb[s - 1])
-                if s < MODELS:
-                    store(s - 1, 0, 1)
-                else:
-                    store(s - 1, 1, 1)
             if 0 <= s + 2 < MODELS:
                 quantise_embedding(s + 2, e_words[s + 2])
             if 0 <= s + 2 < MODELS:
                 a_banks[s + 2] = first_product(s + 2)
+            if 0 <= s < MODELS:
+                g_codes = quantise_hidden(g_words[s])
+            if 1 <= s <= 5:
+                finish(s - 1)
+            if 0 <= s < MODELS:
+                o_banks[s] = second_product(s, *g_codes)
             if 0 <= s + 1 < MODELS:
                 g_planes[s + 1] = gelu(s + 1, a_banks[s + 1])
+            if 0 <= s + 1 < MODELS:
+                g_words[s + 1] = regroup(s + 1, g_planes[s + 1])
+            if 5 <= s < MODELS:
+                finish(s)
             if s + 3 < MODELS and s != -2:
                 e_words[s + 3] = words_of(s + 3, e_banks[s + 3])
             if s == -3:

@@ -22,9 +22,11 @@ TOKENS = P * PATCHES
 QUADRANTS = 4
 PLANES = 4
 
-VECTOR_EMBEDS = ((0, 0), (0, 1))
+VECTOR_EMBEDS = ((0, 0), (0, 1), (3, 0),)
 CHUNK = 4
 WARM_UPS = 4
+LATE = (6,)
+SPLIT_REGROUPS = (7,)
 GPSIMD_REGROUPS = (3, 4, 5, 6,)
 
 FLOPS = 2 * MODELS * TOKENS * (P * D + 2 * D * D)
@@ -252,10 +254,13 @@ def tile_model_pa_e_kernel(
             if n in GPSIMD_REGROUPS:
                 nc.gpsimd.tensor_scalar(out=g_words[:], in0=by_token, scalar1=1.0, scalar2=0.0, op0=MULT, op1=ADD)
             else:
+                cut = P if n in SPLIT_REGROUPS else TOKENS
                 nc.vector.tensor_copy(
-                    out=g_words[:].rearrange("p (c i) t -> p c t i", i=CHUNK),
-                    in_=g_planes[:].rearrange("p t (c i) -> p c t i", i=CHUNK),
+                    out=g_words[:, 0:cut, :].rearrange("p (c i) t -> p c t i", i=CHUNK),
+                    in_=g_planes[:, :, 0:cut].rearrange("p t (c i) -> p c t i", i=CHUNK),
                 )
+                if cut < TOKENS:
+                    nc.scalar.copy(out=g_words[:, cut:, :], in_=by_token[:, cut:, :])
             return g_words
 
         def quantise_hidden(g_words):
@@ -269,7 +274,8 @@ def tile_model_pa_e_kernel(
         def second_product(n, g_codes, g_scales):
             banks = []
             for l in range(PATCHES):
-                o_ps = psum_o.tile([P, D], F32, tag="o")
+                pool, tag = (psum_a, "a") if n in LATE else (psum_o, "o")
+                o_ps = pool.tile([P, D], F32, name="o_ps", tag=tag)
                 tokens = slice(P * l, P * (l + 1))
                 nc.tensor.matmul_mx(
                     out=o_ps[:],
@@ -301,16 +307,17 @@ def tile_model_pa_e_kernel(
         e_banks[0] = embed(0)
         transpose_x(1)
         e_banks[1] = embed(1)
-        def finish(n):
-            o_sb[n] = stage.tile([P, PATCHES, D], F32, name="o_sb", tag="o_sb", bufs=MODELS)
-            for l in range(PATCHES):
-                add_b2(n, l, o_banks[n][l], o_sb[n])
-                if n == MODELS - 1:
-                    store(n, l, l)
-            if n < MODELS - 1:
-                store(n, 0, 1)
+        def add(n, l):
+            if l == 0:
+                o_sb[n] = stage.tile([P, PATCHES, D], F32, name="o_sb", tag="o_sb", bufs=MODELS)
+            add_b2(n, l, o_banks[n][l], o_sb[n])
 
-        for s in range(-3, MODELS):
+        def finish(n):
+            for l in range(PATCHES):
+                add(n, l)
+            store(n, 0, 1)
+
+        for s in range(-3, MODELS - 2):
             if s == -1:
                 load_words(0, 4, 5)
                 load_words(1, 2, 3)
@@ -327,18 +334,20 @@ def tile_model_pa_e_kernel(
                 a_banks[s + 2] = first_product(s + 2)
             if 0 <= s < MODELS:
                 g_codes = quantise_hidden(g_words[s])
-            if 1 <= s <= 5:
+            if 1 <= s:
                 finish(s - 1)
             if 0 <= s < MODELS:
                 o_banks[s] = second_product(s, *g_codes)
             if 0 <= s + 1 < MODELS:
                 g_planes[s + 1] = gelu(s + 1, a_banks[s + 1])
-            if 0 <= s + 1 < MODELS:
-                g_words[s + 1] = regroup(s + 1, g_planes[s + 1])
-            if 5 <= s < MODELS:
-                finish(s)
+            if s == 1:
+                sort_w1_scales(1)
+            if -3 < s and s + 3 < MODELS:
+                sort_w1_codes(s + 3)
             if s + 3 < MODELS and s != -2:
                 e_words[s + 3] = words_of(s + 3, e_banks[s + 3])
+            if 0 <= s + 1 < MODELS:
+                g_words[s + 1] = regroup(s + 1, g_planes[s + 1])
             if s == -3:
                 e_words[1] = words_of(1, e_banks[1])
             if s in (-1, 1):
@@ -347,9 +356,28 @@ def tile_model_pa_e_kernel(
                 e_banks[s + 4] = embed(s + 4)
             if s == -3:
                 sort_w1_scales(0)
-            if s == 1:
-                sort_w1_scales(1)
-            if s + 3 < MODELS:
-                sort_w1_codes(s + 3)
-            if s == -3:
+                sort_w1_codes(0)
                 transpose_rows_by_t()
+        g_codes = quantise_hidden(g_words[6])
+        o_banks[6] = second_product(6, *g_codes)
+        g_planes[7] = gelu(7, a_banks[7])
+        g_words[7] = regroup(7, g_planes[7])
+        add(5, 0)
+        store(5, 0, 0)
+        add(5, 1)
+        store(5, 1, 1)
+        g_codes7 = quantise_hidden(g_words[7])
+        add(6, 0)
+        store(6, 0, 0)
+        add(6, 1)
+        store(6, 1, 1)
+        o_banks[7] = second_product(7, *g_codes7)
+        add(7, 0)
+        store(7, 0, 0)
+        for cols in (slice(0, D // 2), slice(D // 2, D)):
+            nc.vector.tensor_tensor(
+                out=o_sb[7][:, 1, cols], in0=o_banks[7][1][:, cols], in1=b2[:, 7, cols], op=ADD
+            )
+            nc.sync.dma_start(
+                out=out[7, :, :, 1, cols].rearrange("b c d -> (b c) d"), in_=o_sb[7][:, 1, cols]
+            )

@@ -99,10 +99,11 @@ def tile_model_pa_e_kernel(
         load_w1_scales(0)
         load_words(0, 0, 0)
         load_words(0, 1, 1)
+        load_words(0, 2, 2)
         load_w2_scales()
         load_words(1, 0, 0)
         nc.sync.dma_start(out=x_sb[:, :, half:], in_=x_rows[:, :, half:])
-        load_words(0, 2, 3)
+        load_words(0, 3, 3)
         load_b2(0, 3)
         load_words(1, 1, 1)
         load_w1_scales(1)
@@ -350,8 +351,8 @@ def tile_model_pa_e_kernel(
                 g_words[s + 1] = regroup(s + 1, g_planes[s + 1])
             if s == -3:
                 e_words[1] = words_of(1, e_banks[1])
-            if s in (-1, 1):
-                transpose_x(2 + (s + 1) // 2)
+            for pair in {-1: (2,), 0: (3,)}.get(s, ()):
+                transpose_x(pair)
             if 2 <= s + 4 < MODELS:
                 e_banks[s + 4] = embed(s + 4)
             if s == -3:

@@ -22,7 +22,7 @@ TOKENS = P * PATCHES
 QUADRANTS = 4
 PLANES = 4
 
-VECTOR_EMBEDS = ((0, 0), (0, 1), (3, 0),)
+VECTOR_EMBEDS = ((0, 0), (0, 1), (2, 0), (3, 0),)
 CHUNK = 4
 WARM_UPS = 4
 LATE = (6,)
@@ -94,10 +94,9 @@ def tile_model_pa_e_kernel(
         emb_b_col_bf = keep.tile([P, PACK], BF16)
         nc.sync.dma_start(out=x_sb[:, :, 0:half], in_=x_rows[:, :, 0:half])
         nc.sync.dma_start(out=emb_w_sb[:], in_=emb_W)
-        nc.scalar.dma_start(out=emb_b_col_bf[:], in_=emb_b.rearrange("(p t) -> p t", t=PACK))
-        nc.scalar.dma_start(out=rows[0:MODELS, :], in_=enc_b1)
-        load_w1_scales(0)
         load_words(0, 0, 0)
+        load_w1_scales(0)
+        nc.scalar.dma_start(out=emb_b_col_bf[:], in_=emb_b.rearrange("(p t) -> p t", t=PACK))
         load_words(0, 1, 1)
         load_words(0, 2, 2)
         load_w2_scales()
@@ -113,6 +112,7 @@ def tile_model_pa_e_kernel(
         make_identity(nc, ident[:])
         ident_f32 = keep.tile([P, P], F32)
         make_identity(nc, ident_f32[:])
+        nc.gpsimd.dma_start(out=rows[0:MODELS, :], in_=enc_b1)
 
         warm_up = psum_a.tile([P, D], F32, name="warm_up", tag="a")
         for i in range(WARM_UPS):
@@ -129,7 +129,8 @@ def tile_model_pa_e_kernel(
         b1_col = keep.tile([P, PACK, MODELS], F32)
 
         def transpose_x(pair):
-            x_t_ps = psum_e.tile([P, 2 * PATCHES, P], BF16, tag="e")
+            pool, tag = ((psum_a, "a"), (psum_a, "a"), (psum_o, "o"), (psum_e, "e"))[pair]
+            x_t_ps = pool.tile([P, 2 * PATCHES, P], BF16, name="x_t_ps", tag=tag)
             for m in range(2):
                 for l in range(PATCHES):
                     n = 2 * pair + m
@@ -301,8 +302,9 @@ def tile_model_pa_e_kernel(
 
         e_banks, e_words, a_banks, g_planes, g_words, o_banks, o_sb = {}, {}, {}, {}, {}, {}, {}
 
-        nc.vector.tensor_copy(out=emb_w_sorted[:], in_=emb_w_sb[:].rearrange("s (p t) -> s t p", t=PACK))
         nc.vector.tensor_copy(out=emb_b_col[:], in_=emb_b_col_bf[:])
+        nc.vector.tensor_copy(out=emb_w_sorted[:], in_=emb_w_sb[:].rearrange("s (p t) -> s t p", t=PACK))
+        sort_w1_codes(0)
         transpose_x(0)
         spread_emb_b()
         e_banks[0] = embed(0)
@@ -357,7 +359,6 @@ def tile_model_pa_e_kernel(
                 e_banks[s + 4] = embed(s + 4)
             if s == -3:
                 sort_w1_scales(0)
-                sort_w1_codes(0)
                 transpose_rows_by_t()
         g_codes = quantise_hidden(g_words[6])
         o_banks[6] = second_product(6, *g_codes)

@@ -94,25 +94,25 @@ def tile_model_pa_e_kernel(
         emb_b_col_bf = keep.tile([P, PACK], BF16)
         nc.sync.dma_start(out=x_sb[:, :, 0:half], in_=x_rows[:, :, 0:half])
         nc.sync.dma_start(out=emb_w_sb[:], in_=emb_W)
-        load_words(0, 0, 0)
-        load_w1_scales(0)
         nc.scalar.dma_start(out=emb_b_col_bf[:], in_=emb_b.rearrange("(p t) -> p t", t=PACK))
+        load_w1_scales(0)
+        load_words(0, 0, 0)
         load_words(0, 1, 1)
         load_words(0, 2, 2)
         load_w2_scales()
         load_words(1, 0, 0)
         nc.sync.dma_start(out=x_sb[:, :, half:], in_=x_rows[:, :, half:])
+        load_b2(0, 1)
         load_words(0, 3, 3)
-        load_b2(0, 3)
-        load_words(1, 1, 1)
         load_w1_scales(1)
+        load_words(1, 1, 1)
 
         nc.scalar.activation(out=warm[:], in_=warm[:], func=GELU)
         ident = keep.tile([P, P], BF16)
         make_identity(nc, ident[:])
+        nc.gpsimd.dma_start(out=rows[0:MODELS, :], in_=enc_b1)
         ident_f32 = keep.tile([P, P], F32)
         make_identity(nc, ident_f32[:])
-        nc.gpsimd.dma_start(out=rows[0:MODELS, :], in_=enc_b1)
 
         warm_up = psum_a.tile([P, D], F32, name="warm_up", tag="a")
         for i in range(WARM_UPS):
@@ -302,9 +302,8 @@ def tile_model_pa_e_kernel(
 
         e_banks, e_words, a_banks, g_planes, g_words, o_banks, o_sb = {}, {}, {}, {}, {}, {}, {}
 
-        nc.vector.tensor_copy(out=emb_b_col[:], in_=emb_b_col_bf[:])
         nc.vector.tensor_copy(out=emb_w_sorted[:], in_=emb_w_sb[:].rearrange("s (p t) -> s t p", t=PACK))
-        sort_w1_codes(0)
+        nc.vector.tensor_copy(out=emb_b_col[:], in_=emb_b_col_bf[:])
         transpose_x(0)
         spread_emb_b()
         e_banks[0] = embed(0)
@@ -325,27 +324,29 @@ def tile_model_pa_e_kernel(
                 load_words(0, 4, 5)
                 load_words(1, 2, 3)
             if s == 0:
-                load_b2(4, 7)
+                load_b2(2, 7)
             if s == 1:
                 load_words(0, 6, 7)
                 load_words(1, 4, 5)
             if s == 3:
                 load_words(1, 6, 7)
+            if s == 2:
+                sort_w1_scales(1)
             if 0 <= s + 2 < MODELS:
                 quantise_embedding(s + 2, e_words[s + 2])
             if 0 <= s + 2 < MODELS:
                 a_banks[s + 2] = first_product(s + 2)
             if 0 <= s < MODELS:
                 g_codes = quantise_hidden(g_words[s])
+            if 4 <= s and s + 3 < MODELS:
+                sort_w1_codes(s + 3)
             if 1 <= s:
                 finish(s - 1)
             if 0 <= s < MODELS:
                 o_banks[s] = second_product(s, *g_codes)
             if 0 <= s + 1 < MODELS:
                 g_planes[s + 1] = gelu(s + 1, a_banks[s + 1])
-            if s == 1:
-                sort_w1_scales(1)
-            if -3 < s and s + 3 < MODELS:
+            if -3 < s < 4:
                 sort_w1_codes(s + 3)
             if s + 3 < MODELS and s != -2:
                 e_words[s + 3] = words_of(s + 3, e_banks[s + 3])
@@ -358,16 +359,17 @@ def tile_model_pa_e_kernel(
             if 2 <= s + 4 < MODELS:
                 e_banks[s + 4] = embed(s + 4)
             if s == -3:
+                sort_w1_codes(0)
                 sort_w1_scales(0)
                 transpose_rows_by_t()
-        g_codes = quantise_hidden(g_words[6])
-        o_banks[6] = second_product(6, *g_codes)
-        g_planes[7] = gelu(7, a_banks[7])
-        g_words[7] = regroup(7, g_planes[7])
         add(5, 0)
         store(5, 0, 0)
         add(5, 1)
         store(5, 1, 1)
+        g_codes = quantise_hidden(g_words[6])
+        o_banks[6] = second_product(6, *g_codes)
+        g_planes[7] = gelu(7, a_banks[7])
+        g_words[7] = regroup(7, g_planes[7])
         g_codes7 = quantise_hidden(g_words[7])
         add(6, 0)
         store(6, 0, 0)

from contextlib import ExitStack

import concourse.mybir as mybir
from concourse.masks import make_identity

F32 = mybir.dt.float32
BF16 = mybir.dt.bfloat16
I32 = mybir.dt.int32
U32 = mybir.dt.uint32
U8 = mybir.dt.uint8
FP8X4 = mybir.dt.float8_e4m3fn_x4
ADD = mybir.AluOpType.add
MULT = mybir.AluOpType.mult
GELU = mybir.ActivationFunctionType.Gelu_apprx_tanh

P = 128
PACK = 4
D = P * PACK
MODELS = 8
PATCHES = 2
TOKENS = P * PATCHES
QUADRANTS = 4
PLANES = 4

VECTOR_EMBEDS = ((0, 0), (0, 1), (2, 0), (3, 0),)
CHUNK = 4
WARM_UPS = 4
LATE = (6,)
SPLIT_REGROUPS = (7,)
GPSIMD_REGROUPS = (3, 4, 5, 6,)

FLOPS = 2 * MODELS * TOKENS * (P * D + 2 * D * D)


def tile_model_pa_e_kernel(
    tc, x, emb_W, emb_b, enc_W1_words, enc_W1_scales, enc_b1, enc_W2_words, enc_W2_scales, enc_b2, out
):
    nc = tc.nc
    with ExitStack() as ctx:
        ctx.enter_context(tc.manual_schedule())
        keep = ctx.enter_context(tc.tile_pool(name="keep", bufs=1))
        stage = ctx.enter_context(tc.tile_pool(name="stage", bufs=3))
        psum_a = ctx.enter_context(tc.psum_pool(name="psum_a", bufs=4))
        psum_o = ctx.enter_context(tc.psum_pool(name="psum_o", bufs=2))
        psum_e = ctx.enter_context(tc.psum_pool(name="psum_e", bufs=2))

        zeros = keep.tile([P, D], BF16)
        nc.vector.memset(zeros[:].bitcast(I32), 0)
        rows = keep.tile([P, D], BF16)
        nc.vector.memset(rows[:].bitcast(I32), 0)
        raw_scales = keep.tile([P, 2, D], U8, align_bytes=64)
        nc.vector.memset(raw_scales[:].rearrange("p g c -> p (g c)").bitcast(I32), 0)
        w2_scales = keep.tile([P, MODELS, D], U8, align_bytes=64)
        nc.vector.memset(w2_scales[:].rearrange("p n c -> p (n c)").bitcast(I32), 0)
        warm = keep.tile([P, 1], F32)
        nc.vector.memset(warm[:], 0.0)

        words = keep.tile([P, 2, MODELS, D], I32, align_bytes=64)

        def load_w1_scales(half):
            first = PLANES * half
            for q in range(QUADRANTS):
                nc.sync.dma_start(
                    out=raw_scales[32 * q : 32 * q + 4 * PLANES, half, :].bitcast(I32),
                    in_=enc_W1_scales[first : first + PLANES, 4 * q : 4 * q + 4, :].bitcast(I32),
                )

        def load_w2_scales():
            for q in range(QUADRANTS):
                nc.sync.dma_start(
                    out=w2_scales[32 * q : 32 * q + 4, :, :].bitcast(I32),
                    in_=enc_W2_scales.bitcast(I32)[:, 4 * q : 4 * q + 4, :].rearrange("g r c -> r g c"),
                )

        def load_words(layer, first, last):
            given = (enc_W1_words, enc_W2_words)[layer]
            nc.sync.dma_start(
                out=words[:, layer, first : last + 1, :],
                in_=given[first : last + 1].rearrange("g p c t -> p g (c t)").bitcast(I32),
            )

        b2 = keep.tile([P, MODELS, D], BF16)

        def load_b2(first, last):
            nc.sync.dma_start(
                out=b2[:, first : last + 1, :].rearrange("p n d -> p (n d)"),
                in_=enc_b2[first : last + 1, :].rearrange("n d -> (n d)").partition_broadcast(P),
            )

        x_sb = keep.tile([P, PATCHES, MODELS * P], BF16)
        x_rows = x.rearrange("b c (l t) -> (b c) l t", l=PATCHES)
        half = MODELS // 2 * P
        emb_w_sb = keep.tile([P, D], BF16)
        emb_b_col_bf = keep.tile([P, PACK], BF16)
        nc.sync.dma_start(out=x_sb[:, :, 0:half], in_=x_rows[:, :, 0:half])
        nc.sync.dma_start(out=emb_w_sb[:], in_=emb_W)
        nc.scalar.dma_start(out=emb_b_col_bf[:], in_=emb_b.rearrange("(p t) -> p t", t=PACK))
        load_w1_scales(0)
        load_words(0, 0, 0)
        load_words(0, 1, 1)
        load_words(0, 2, 2)
        load_w2_scales()
        load_words(1, 0, 0)
        nc.sync.dma_start(out=x_sb[:, :, half:], in_=x_rows[:, :, half:])
        load_b2(0, 1)
        load_words(0, 3, 3)
        load_w1_scales(1)
        load_words(1, 1, 1)

        nc.scalar.activation(out=warm[:], in_=warm[:], func=GELU)
        ident = keep.tile([P, P], BF16)
        make_identity(nc, ident[:])
        nc.gpsimd.dma_start(out=rows[0:MODELS, :], in_=enc_b1)
        ident_f32 = keep.tile([P, P], F32)
        make_identity(nc, ident_f32[:])

        warm_up = psum_a.tile([P, D], F32, name="warm_up", tag="a")
        for i in range(WARM_UPS):
            nc.tensor.matmul(out=warm_up[:], lhsT=zeros[:, 0:P], rhs=zeros[:], start=True, stop=True)
        x_t = keep.tile([P, MODELS * TOKENS], BF16)
        e_codes = keep.tile([P, MODELS, TOKENS], U32, align_bytes=64)
        e_scales = keep.tile([P, MODELS, TOKENS], U8, align_bytes=64)
        w1_codes = keep.tile([P, MODELS, D], I32, align_bytes=64)
        w1_scales = keep.tile([P, 2, D], U8, align_bytes=64)

        emb_b_rows = keep.tile([P, PACK, P], F32)
        emb_w_sorted = keep.tile([P, PACK, P], BF16)
        emb_b_col = keep.tile([P, PACK], F32)
        b1_col = keep.tile([P, PACK, MODELS], F32)

        def transpose_x(pair):
            pool, tag = ((psum_a, "a"), (psum_a, "a"), (psum_o, "o"), (psum_e, "e"))[pair]
            x_t_ps = pool.tile([P, 2 * PATCHES, P], BF16, name="x_t_ps", tag=tag)
            for m in range(2):
                for l in range(PATCHES):
                    n = 2 * pair + m
                    nc.tensor.transpose(
                        out=x_t_ps[:, PATCHES * m + l, :], in_=x_sb[:, l, P * n : P * (n + 1)], identity=ident[:]
                    )
            nc.scalar.copy(
                out=x_t[:, 2 * TOKENS * pair : 2 * TOKENS * (pair + 1)], in_=x_t_ps[:].rearrange("s a b -> s (a b)")
            )

        def spread_emb_b():
            ps = psum_a.tile([P, PACK, P], F32, tag="a")
            for t in range(PACK):
                nc.tensor.transpose(
                    out=ps[:, t, :], in_=emb_b_col[:, t : t + 1].to_broadcast([P, P]), identity=ident_f32[:]
                )
            nc.scalar.copy(out=emb_b_rows[:], in_=ps[:])

        def transpose_rows_by_t():
            ps = psum_a.tile([P, PACK, P], BF16, tag="a")
            for t in range(PACK):
                nc.tensor.transpose(out=ps[:, t, :], in_=rows[:].rearrange("r (p t) -> r t p", t=PACK)[:, t, :], identity=ident[:])
            nc.scalar.copy(out=b1_col[:], in_=ps[:, :, 0:MODELS])


        def multiply_patches(n, l, bank, alone):
            first = TOKENS * n + P * l
            for t in range(PACK):
                nc.tensor.matmul(
                    out=bank[:, t, :],
                    lhsT=emb_w_sorted[:, t, :],
                    rhs=x_t[:, first : first + P],
                    start=alone,
                    stop=alone or t == PACK - 1,
                )

        def embed(n):
            pool, tag = (psum_o, "o") if n == 0 else (psum_e, "e")
            banks = [pool.tile([P, PACK, P], F32, name="e_ps", tag=tag) for l in range(PATCHES)]
            seeded = [(n, l) not in VECTOR_EMBEDS for l in range(PATCHES)]
            for l in range(PATCHES):
                if not seeded[l]:
                    multiply_patches(n, l, banks[l], True)
            for l in range(PATCHES):
                if seeded[l]:
                    for t in range(PACK):
                        nc.tensor.matmul(
                            out=banks[l][:, t, :],
                            lhsT=emb_b_rows[:, t, :],
                            rhs=ident_f32[:],
                            start=t == 0,
                            stop=False,
                            is_transpose=True,
                        )
            for l in range(PATCHES):
                if seeded[l]:
                    multiply_patches(n, l, banks[l], False)
            return banks

        def words_of(n, banks):
            e_words = stage.tile([P, TOKENS, PACK], BF16, align_bytes=64)
            for l in range(PATCHES):
                part = e_words[:, P * l : P * (l + 1), :]
                by_token = banks[l][:].rearrange("p t w -> p w t")
                if (n, l) in VECTOR_EMBEDS:
                    nc.vector.tensor_tensor(
                        out=part,
                        in0=by_token,
                        in1=emb_b_col[:].unsqueeze(1).to_broadcast([P, P, PACK]),
                        op=ADD,
                    )
                else:
                    nc.scalar.copy(out=part, in_=by_token)
            return e_words

        def quantise_embedding(n, e_words):
            nc.vector.quantize_mx(
                out=e_codes[:, n, :].bitcast(FP8X4), scales=e_scales[:, n, :], in_=e_words[:].rearrange("p w t -> p (w t)")
            )

        def sort_w1_codes(n):
            nc.vector.tensor_copy(
                out=w1_codes[:, n, :].rearrange("p (t c) -> p t c", t=PACK),
                in_=words[:, 0, n, :].rearrange("p (c t) -> p t c", t=PACK),
            )

        def sort_w1_scales(half):
            nc.vector.tensor_copy(
                out=w1_scales[:, half, :].rearrange("p (t c) -> p c t", t=PACK),
                in_=raw_scales[:, half, :].rearrange("p (c t) -> p c t", t=PACK),
            )

        def first_product(n):
            plane = 4 * (n % PLANES)
            banks = []
            for pair in range(2):
                a_ps = psum_a.tile([P, 2, TOKENS], F32, tag="a")
                for i in range(2):
                    cols = slice(P * (2 * pair + i), P * (2 * pair + i + 1))
                    nc.tensor.matmul_mx(
                        out=a_ps[:, i, :],
                        lhsT=w1_codes[:, n, cols].bitcast(FP8X4),
                        lhsT_scale=w1_scales[plane:P, n // PLANES, cols],
                        rhs=e_codes[:, n, :].bitcast(FP8X4),
                        rhs_scale=e_scales[:, n, :],
                        start=True,
                        stop=True,
                    )
                banks.append(a_ps)
            return banks

        def gelu(n, banks):
            g_planes = stage.tile([P, PACK, TOKENS], BF16)
            for t in range(PACK):
                nc.scalar.activation(
                    out=g_planes[:, t, :], in_=banks[t // 2][:, t % 2, :], func=GELU, bias=b1_col[:, t, n : n + 1], scale=1.0
                )
            return g_planes

        def regroup(n, g_planes):
            g_words = stage.tile([P, TOKENS, PACK], BF16, align_bytes=64)
            by_token = g_planes[:].rearrange("p t w -> p w t")
            if n in GPSIMD_REGROUPS:
                nc.gpsimd.tensor_scalar(out=g_words[:], in0=by_token, scalar1=1.0, scalar2=0.0, op0=MULT, op1=ADD)
            else:
                cut = P if n in SPLIT_REGROUPS else TOKENS
                nc.vector.tensor_copy(
                    out=g_words[:, 0:cut, :].rearrange("p (c i) t -> p c t i", i=CHUNK),
                    in_=g_planes[:, :, 0:cut].rearrange("p t (c i) -> p c t i", i=CHUNK),
                )
                if cut < TOKENS:
                    nc.scalar.copy(out=g_words[:, cut:, :], in_=by_token[:, cut:, :])
            return g_words

        def quantise_hidden(g_words):
            g_codes = stage.tile([P, TOKENS], U32, align_bytes=64)
            g_scales = stage.tile([P, TOKENS], U8, align_bytes=64)
            nc.vector.quantize_mx(
                out=g_codes[:].bitcast(FP8X4), scales=g_scales[:], in_=g_words[:].rearrange("p w t -> p (w t)")
            )
            return g_codes, g_scales

        def second_product(n, g_codes, g_scales):
            banks = []
            for l in range(PATCHES):
                pool, tag = (psum_a, "a") if n in LATE else (psum_o, "o")
                o_ps = pool.tile([P, D], F32, name="o_ps", tag=tag)
                tokens = slice(P * l, P * (l + 1))
                nc.tensor.matmul_mx(
                    out=o_ps[:],
                    lhsT=g_codes[:, tokens].bitcast(FP8X4),
                    lhsT_scale=g_scales[:, tokens],
                    rhs=words[:, 1, n, :].bitcast(FP8X4),
                    rhs_scale=w2_scales[:, n, :],
                    start=True,
                    stop=True,
                )
                banks.append(o_ps)
            return banks

        def add_b2(n, l, o_ps, o_sb):
            nc.vector.tensor_tensor(out=o_sb[:, l, :], in0=o_ps[:], in1=b2[:, n, :], op=ADD)

        def store(n, first, last):
            nc.sync.dma_start(
                out=out[n, :, :, first : last + 1, :].rearrange("b c l d -> (b c) l d"), in_=o_sb[n][:, first : last + 1, :]
            )


        e_banks, e_words, a_banks, g_planes, g_words, o_banks, o_sb = {}, {}, {}, {}, {}, {}, {}

        nc.vector.tensor_copy(out=emb_w_sorted[:], in_=emb_w_sb[:].rearrange("s (p t) -> s t p", t=PACK))
        nc.vector.tensor_copy(out=emb_b_col[:], in_=emb_b_col_bf[:])
        transpose_x(0)
        spread_emb_b()
        e_banks[0] = embed(0)
        transpose_x(1)
        e_banks[1] = embed(1)
        def add(n, l):
            if l == 0:
                o_sb[n] = stage.tile([P, PATCHES, D], F32, name="o_sb", tag="o_sb", bufs=MODELS)
            add_b2(n, l, o_banks[n][l], o_sb[n])

        def finish(n):
            for l in range(PATCHES):
                add(n, l)
            store(n, 0, 1)

        for s in range(-3, MODELS - 2):
            if s == -1:
                load_words(0, 4, 5)
                load_words(1, 2, 3)
            if s == 0:
                load_b2(2, 7)
            if s == 1:
                load_words(0, 6, 7)
                load_words(1, 4, 5)
            if s == 3:
                load_words(1, 6, 7)
            if s == 2:
                sort_w1_scales(1)
            if 0 <= s + 2 < MODELS:
                quantise_embedding(s + 2, e_words[s + 2])
            if 0 <= s + 2 < MODELS:
                a_banks[s + 2] = first_product(s + 2)
            if 0 <= s < MODELS:
                g_codes = quantise_hidden(g_words[s])
            if 4 <= s and s + 3 < MODELS:
                sort_w1_codes(s + 3)
            if 1 <= s:
                finish(s - 1)
            if 0 <= s < MODELS:
                o_banks[s] = second_product(s, *g_codes)
            if 0 <= s + 1 < MODELS:
                g_planes[s + 1] = gelu(s + 1, a_banks[s + 1])
            if -3 < s < 4:
                sort_w1_codes(s + 3)
            if s + 3 < MODELS and s != -2:
                e_words[s + 3] = words_of(s + 3, e_banks[s + 3])
            if 0 <= s + 1 < MODELS:
                g_words[s + 1] = regroup(s + 1, g_planes[s + 1])
            if s == -3:
                e_words[1] = words_of(1, e_banks[1])
            for pair in {-1: (2,), 0: (3,)}.get(s, ()):
                transpose_x(pair)
            if 2 <= s + 4 < MODELS:
                e_banks[s + 4] = embed(s + 4)
            if s == -3:
                sort_w1_codes(0)
                sort_w1_scales(0)
                transpose_rows_by_t()
        add(5, 0)
        store(5, 0, 0)
        add(5, 1)
        store(5, 1, 1)
        g_codes = quantise_hidden(g_words[6])
        o_banks[6] = second_product(6, *g_codes)
        g_planes[7] = gelu(7, a_banks[7])
        g_words[7] = regroup(7, g_planes[7])
        g_codes7 = quantise_hidden(g_words[7])
        add(6, 0)
        store(6, 0, 0)
        add(6, 1)
        store(6, 1, 1)
        o_banks[7] = second_product(7, *g_codes7)
        add(7, 0)
        store(7, 0, 0)
        for cols in (slice(0, D // 2), slice(D // 2, D)):
            nc.vector.tensor_tensor(
                out=o_sb[7][:, 1, cols], in0=o_banks[7][1][:, cols], in1=b2[:, 7, cols], op=ADD
            )
            nc.sync.dma_start(
                out=out[7, :, :, 1, cols].rearrange("b c d -> (b c) d"), in_=o_sb[7][:, 1, cols]
            )
